import numpy as np
import ml_dtypes


def mxq(x, axis, fmt="e4m3"):
    dtype, down = {"e4m3": (ml_dtypes.float8_e4m3fn, 7), "e5m2": (ml_dtypes.float8_e5m2, 14)}[fmt]
    v = np.moveaxis(np.asarray(x, np.float32).astype(ml_dtypes.bfloat16).astype(np.float64), axis, -1)
    blocks = v.reshape(v.shape[:-1] + (-1, 32))
    amax = np.abs(blocks).max(-1, keepdims=True)
    byte = np.maximum(np.where(amax > 0, np.frexp(amax)[1] - 1 + 127, 0) - down, 1)
    scale = np.exp2(byte - 127.0)
    codes = (blocks / scale).astype(np.float32).astype(dtype).astype(np.float64)
    return np.moveaxis((codes * scale).reshape(v.shape), -1, axis)


WIDE = False


def mx_kscale(k):
    if not WIDE:
        return np.ones(k)
    levels = np.array([10, -10, 5, -5, 0])
    a = np.random.permutation(np.resize(levels, k // 512 * 4)).reshape(k // 512, 4)
    idx = np.arange(k)
    return np.exp2(a[idx // 512, idx % 128 // 32])


BF16 = ml_dtypes.bfloat16


def bf(x):
    return np.asarray(x, np.float32).astype(BF16)


def f64(x):
    return np.asarray(x).astype(np.float64)


B, F, H, C = 1024, 1024, 512, 10
EPS = 4.0 / 30.0
P_KEEP = 0.95


def setup_inputs():
    s = mx_kscale(F)
    ns = EPS / (6.0 * np.sqrt(H))
    return {"x1": bf(np.random.standard_normal((B, F)) * s),
            "x2": bf(np.random.standard_normal((B, F)) * s),
            "W1": bf(np.random.standard_normal((F, H)) / np.sqrt(F) / s[:, None]),
            "b1": bf(np.random.standard_normal(H) * 0.3),
            "W2": bf(np.random.standard_normal((F, H)) / np.sqrt(F) / s[:, None]),
            "b2": bf(np.random.standard_normal(H) * 0.3),
            "noise_std": bf(np.random.laplace(size=(B, H)) * ns),
            "rr_uniform": bf(np.random.uniform(size=H))}


def reference(x1, x2, W1, b1, W2, b2, noise_std, rr_uniform):
    out1 = (mxq(f64(x1), 1, "e4m3") @ mxq(f64(W1), 0, "e4m3")) + f64(b1)
    one_norm = np.sum(np.abs(out1), axis=1)
    sensitivity = np.max(one_norm) - np.min(one_norm)
    noise_mul = sensitivity / EPS
    out1 = out1 + f64(noise_std) * noise_mul
    rr_mask = np.where(f64(rr_uniform) < P_KEEP, 1.0, 0.0)
    out1 = out1 * rr_mask
    out2 = (mxq(f64(x2), 1, "e4m3") @ mxq(f64(W2), 0, "e4m3")) + f64(b2)
    return np.minimum(out1, out2)

@@ -1,0 +1,283 @@
+from contextlib import ExitStack
+
+import concourse.mybir as mybir
+from concourse.masks import make_identity
+
+F32 = mybir.dt.float32
+BF16 = mybir.dt.bfloat16
+U32 = mybir.dt.uint32
+U8 = mybir.dt.uint8
+FP8X4 = mybir.dt.float8_e4m3fn_x4
+ALU = mybir.AluOpType
+ACT = mybir.ActivationFunctionType
+AX = mybir.AxisListType
+
+P = 128
+B, F, H = 1024, 1024, 512
+FLOPS = 2 * 2 * B * F * H
+INV_EPS = 7.5
+P_KEEP = 0.95
+
+ON_VECTOR = ('xC04','at00','at01','at02','at03','at12',)
+W2_ENGINE = ('V','V')
+ADD_ENGINE = {'adds1_23':'V'}
+ORDER = (
+    "wR00", "xT00", "vecT", "xT01", "xC00", "vec", "xC01", "wR01", "xT02", "wQ01", "xT03", "xC02",
+    "wQ00", "xC03", "xT04", "xQ02", "xT05", "xQ01", "xC04", "xC05", "xT06", "xQ00", "xT07", "xQ03",
+    "xC06", "m000", "xQ04", "xC07", "xQ06", "m001", "xQ05", "xQ07", "m003", "ab01", "at01", "m002",
+    "ab00", "at00", "m011", "ab03", "at03", "adds0_01", "m012", "at02", "ab02", "m013", "wR10",
+    "adds0_23", "m010", "ab12", "xT11", "ab11", "wQ10", "ns00", "ab10", "at12", "ab13", "adds1_01",
+    "xT10", "wR11", "ns01", "xC11", "xC10", "xQ11", "ns10", "adds1_23", "at10", "xQ10", "red0", "ns11",
+    "wQ11", "xT13", "red1", "xC13", "rmax", "sens", "at13", "nT00", "mk", "xQ13", "xT12", "cT00",
+    "nT01", "xC12", "cT01", "xT14", "xT15", "xC14", "xQ12", "nT10", "cT03", "xC15", "m101", "cT02",
+    "at11", "m100", "oT01", "xT17", "oT00", "xT16", "xC17", "m102", "xQ14", "xC16", "cT10", "m103",
+    "xQ17", "nT11", "xQ16", "xQ15", "oR00", "oT03", "oR01", "oC00", "oT02", "m110", "oC01", "cT11",
+    "oR02", "oT10", "oR03", "oC02", "m111", "cT12", "oC03", "oR10", "oT11", "m112", "oC10", "cT13",
+    "oR11", "oT12", "m113", "oC11", "oR12", "oT13", "oC12", "oR13", "oC13",
+)
+
+
+def tile_splitnn_pa_kernel(tc, x1, x2, W1, b1, W2, b2, noise_std, rr_uniform, out):
+    nc = tc.nc
+    with ExitStack() as ctx:
+        ctx.enter_context(tc.manual_schedule())
+        const = ctx.enter_context(tc.tile_pool(name="const", bufs=1))
+        stage = ctx.enter_context(tc.tile_pool(name="stage", bufs=4))
+        absp = ctx.enter_context(tc.tile_pool(name="absp", bufs=4))
+        sump = ctx.enter_context(tc.tile_pool(name="sump", bufs=3))
+        outp = ctx.enter_context(tc.tile_pool(name="outp", bufs=8))
+        psum = ctx.enter_context(tc.psum_pool(name="psum", bufs=2))
+
+        ident_f = const.tile([P, P], F32)
+        make_identity(nc, ident_f[:])
+        ident_b = const.tile([P, P], BF16)
+        make_identity(nc, ident_b[:])
+        vraw = const.tile([P, P], BF16)
+        nc.vector.memset(vraw[:], 0.0)
+        plusminus = const.tile([P, P], F32)
+        nc.vector.memset(plusminus[:, 0:64], 1.0)
+        nc.vector.memset(plusminus[:, 64:128], -1.0)
+        pick = const.tile([P, P], F32)
+        nc.vector.memset(pick[:], 0.0)
+        nc.vector.memset(pick[0:1, :], 1.0)
+        nc.vector.memset(pick[64:65, :], 1.0)
+        warm = const.tile([P, 1], F32)
+        nc.vector.memset(warm[:], 0.0)
+        warm2 = const.tile([P, 1], F32)
+        nc.scalar.activation(out=warm2[:], in_=warm[:], func=ACT.Abs)
+
+        nc.scalar.dma_start(out=vraw[0:4, :], in_=b1.rearrange("(r c) -> r c", c=P))
+        nc.scalar.dma_start(out=vraw[4:8, :], in_=b2.rearrange("(r c) -> r c", c=P))
+        nc.scalar.dma_start(out=vraw[8:12, :], in_=rr_uniform.rearrange("(r c) -> r c", c=P))
+
+        wraw = [const.tile([P, 2, 4, H], BF16, name="wraw%d" % c) for c in range(2)]
+        xraw = [const.tile([P, 8 * F], BF16, name="xraw%d" % c) for c in range(2)]
+        nraw = const.tile([P, 8, H], BF16)
+
+        def load_w(c, W, g):
+            nc.sync.dma_start(
+                out=wraw[c][:, g].rearrange("q (u e) h -> q u (e h)", u=2),
+                in_=W[512 * g:512 * (g + 1), :].rearrange("(u q e) h -> q u (e h)", u=2, e=2),
+            )
+
+        def load_x(c, x, j):
+            xv = x.rearrange("(p t) k -> p (t k)", t=8)
+            nc.sync.dma_start(out=xraw[c][:, 2048 * j:2048 * (j + 1)], in_=xv[:, 2048 * j:2048 * (j + 1)])
+
+        load_w(0, W1, 0)
+        load_x(0, x1, 0)
+        load_w(0, W1, 1)
+        for j in range(1, 4):
+            load_x(0, x1, j)
+        load_w(1, W2, 0)
+        load_w(1, W2, 1)
+        for j in range(4):
+            load_x(1, x2, j)
+        nc.sync.dma_start(out=nraw[:], in_=noise_std.rearrange("(p t) h -> p t h", t=8))
+
+        vec = const.tile([P, 12], F32)
+        keep = const.tile([P, 4], F32)
+        b1k = const.tile([P, 4], F32)
+        keep_e = const.tile([P, 4], F32)
+        wgrp = [const.tile([P, 2, H, 4], BF16, name="wgrp%d" % c, align_bytes=64) for c in range(2)]
+        wq = [const.tile([P, 2, H], U32, name="wq%d" % c, align_bytes=64) for c in range(2)]
+        ws = [const.tile([P, 2, H], U8, name="ws%d" % c, align_bytes=64) for c in range(2)]
+        xq = [const.tile([P, 2, 2, 512], U32, name="xq%d" % c, align_bytes=64) for c in range(2)]
+        xs = [const.tile([P, 2, 2, 512], U8, name="xs%d" % c, align_bytes=64) for c in range(2)]
+        a_t = const.tile([P, 4, B], F32)
+        r2 = const.tile([P, 2], F32)
+        rr2 = const.tile([P, 2], F32)
+        mk = const.tile([P, 4], F32)
+        osb = const.tile([P, 8, H], F32)
+        outv = out.rearrange("(p t) h -> p t h", t=8)
+        live = {}
+
+        def copy_engine(label):
+            return nc.vector.tensor_copy if label in ON_VECTOR else nc.scalar.copy
+
+        def vec_t():
+            vps = psum.tile([P, P], BF16, tag="nz")
+            live["vps"] = vps
+            nc.tensor.transpose(vps[:], vraw[:], ident_b[:])
+
+        def vec_v():
+            nc.vector.tensor_copy(out=vec[:], in_=live["vps"][:, 0:12])
+            nc.vector.tensor_single_scalar(out=keep[:], in_=vec[:, 8:12], scalar=P_KEEP, op=ALU.is_lt)
+            nc.vector.tensor_tensor(out=b1k[:], in0=vec[:, 0:4], in1=keep[:], op=ALU.mult)
+            nc.vector.tensor_single_scalar(out=keep_e[:], in_=keep[:], scalar=INV_EPS, op=ALU.mult)
+
+        def w_regroup(c, g):
+            dst = wgrp[c][:, g].rearrange("p (c i) t -> p c t i", i=4)
+            src = wraw[c][:, g].rearrange("p t (c i) -> p c t i", i=4)
+            eng = W2_ENGINE[g] if c == 1 else "V"
+            if eng == "V":
+                nc.vector.tensor_copy(out=dst, in_=src)
+            elif eng == "S":
+                nc.scalar.copy(out=dst, in_=src)
+            else:
+                nc.gpsimd.tensor_scalar(out=dst, in0=src, scalar1=1.0, scalar2=0.0, op0=ALU.mult, op1=ALU.add)
+
+        def w_quant(c, g):
+            nc.vector.quantize_mx(
+                out=wq[c][:, g, :].bitcast(FP8X4), scales=ws[c][:, g, :],
+                in_=wgrp[c][:, g].rearrange("p h t -> p (h t)"),
+            )
+
+        def x_t(c, i):
+            j, g = i // 2, i % 2
+            xw = xraw[c][:].bitcast(F32)
+            xt = psum.tile([P, 2, 2, P], F32, tag=("nz" if (c == 0 and i % 4 >= 2) else "xt"))
+            live["xt%d%d" % (c, i)] = xt
+            for tt in range(2):
+                for u in range(2):
+                    off = 512 * (2 * j + tt) + 256 * g + 128 * u
+                    nc.tensor.transpose(xt[:, tt, u, :], xw[:, off:off + P], ident_f[:])
+
+        def x_c(c, i):
+            stg = stage.tile([P, 1024], BF16, tag="stg", align_bytes=64)
+            live["stg%d%d" % (c, i)] = stg
+            copy_engine("xC%d%d" % (c, i))(
+                out=stg[:].bitcast(F32).rearrange("q (tt r u) -> q tt r u", tt=2, u=2),
+                in_=live["xt%d%d" % (c, i)][:].rearrange("q tt u r -> q tt r u"),
+            )
+
+        def x_q(c, i):
+            j, g = i // 2, i % 2
+            col = 256 * (j % 2)
+            nc.vector.quantize_mx(
+                out=xq[c][:, j // 2, g, col:col + 256].bitcast(FP8X4),
+                scales=xs[c][:, j // 2, g, col:col + 256],
+                in_=live["stg%d%d" % (c, i)][:],
+            )
+
+        def mx(c, hf, ht):
+            acc = psum.tile([P, 512], F32, tag=("ot" if (c == 0 and ht % 2 == 1) else "acc"))
+            live["acc%d%d%d" % (c, hf, ht)] = acc
+            for g in range(2):
+                nc.tensor.matmul_mx(
+                    out=acc[:],
+                    lhsT=wq[c][:, g, P * ht:P * (ht + 1)].bitcast(FP8X4),
+                    lhsT_scale=ws[c][:, g, P * ht:P * (ht + 1)],
+                    rhs=xq[c][:, hf, g, :].bitcast(FP8X4),
+                    rhs_scale=xs[c][:, hf, g, :],
+                    start=(g == 0), stop=(g == 1),
+                )
+
+        def ab(hf, ht):
+            t = absp.tile([P, 512], F32, tag="ab")
+            live["ab%d%d" % (hf, ht)] = t
+            nc.scalar.activation(out=t[:], in_=live["acc0%d%d" % (hf, ht)][:], func=ACT.Abs,
+                                 bias=vec[:, ht:ht + 1], scale=1.0)
+
+        def at(hf, ht):
+            dst = a_t[:, ht, 512 * hf:512 * (hf + 1)]
+            src = live["acc0%d%d" % (hf, ht)][:]
+            if ("at%d%d" % (hf, ht)) in ON_VECTOR:
+                nc.vector.tensor_scalar(out=dst, in0=src, scalar1=keep[:, ht:ht + 1], scalar2=b1k[:, ht:ht + 1],
+                                        op0=ALU.mult, op1=ALU.add)
+            else:
+                nc.scalar.activation(out=dst, in_=src, func=ACT.Identity, bias=b1k[:, ht:ht + 1],
+                                     scale=keep[:, ht:ht + 1])
+
+        def add(hf, pair):
+            t = sump.tile([P, 512], F32, tag="s")
+            live["s%d%d" % (hf, pair)] = t
+            eng = nc.vector if ADD_ENGINE.get("adds%d_%d%d" % (hf, 2 * pair, 2 * pair + 1), "G") == "V" else nc.gpsimd
+            eng.tensor_tensor(out=t[:], in0=live["ab%d%d" % (hf, 2 * pair)][:],
+                              in1=live["ab%d%d" % (hf, 2 * pair + 1)][:], op=ALU.add)
+
+        def ns(hf, pair):
+            if pair == 0:
+                live["ns%d" % hf] = psum.tile([P, 512], F32, tag="nz", name="ns")
+            nc.tensor.matmul(out=live["ns%d" % hf][:], lhsT=plusminus[:], rhs=live["s%d%d" % (hf, pair)][:],
+                             start=(pair == 0), stop=(pair == 1))
+
+        def red(hf):
+            nc.vector.tensor_reduce(out=r2[:, hf:hf + 1], in_=live["ns%d" % hf][:], axis=AX.X, op=ALU.max)
+
+        def rmax():
+            nc.vector.tensor_tensor(out=rr2[:], in0=r2[:, 0:1].to_broadcast([P, 2]),
+                                    in1=r2[:, 1:2].to_broadcast([P, 2]), op=ALU.max)
+
+        def sens():
+            live["sens"] = psum.tile([P, 2], F32, tag="nz", name="sens")
+            nc.tensor.matmul(out=live["sens"][:], lhsT=pick[:], rhs=rr2[:], start=True, stop=True)
+
+        def mk_v():
+            nc.vector.tensor_tensor(out=mk[:], in0=live["sens"][:, 0:1].to_broadcast([P, 4]), in1=keep_e[:],
+                                    op=ALU.mult)
+
+        def n_t(hf, hp):
+            nz = psum.tile([P, 2, 512], BF16, tag="nz")
+            live["nz%d%d" % (hf, hp)] = nz
+            for a in range(2):
+                ht = 2 * hp + a
+                for tt in range(4):
+                    nc.tensor.transpose(nz[:, a, P * tt:P * (tt + 1)],
+                                        nraw[:, 4 * hf + tt, P * ht:P * (ht + 1)], ident_b[:])
+
+        def c_t(hf, ht):
+            sl = a_t[:, ht, 512 * hf:512 * (hf + 1)]
+            nc.vector.scalar_tensor_tensor(out=sl, in0=live["nz%d%d" % (hf, ht // 2)][:, ht % 2, :],
+                                           scalar=mk[:, ht:ht + 1], in1=sl, op0=ALU.mult, op1=ALU.add)
+
+        def o_t(hf, ht):
+            t = outp.tile([P, 512], F32, tag="o_t")
+            live["oT%d%d" % (hf, ht)] = t
+            nc.vector.scalar_tensor_tensor(out=t[:], in0=live["acc1%d%d" % (hf, ht)][:],
+                                           scalar=vec[:, 4 + ht:5 + ht],
+                                           in1=a_t[:, ht, 512 * hf:512 * (hf + 1)], op0=ALU.add, op1=ALU.min)
+
+        def o_tr(hf, ht):
+            ot = psum.tile([P, 4, P], F32, tag="ot")
+            live["ot%d%d" % (hf, ht)] = ot
+            for tt in range(4):
+                nc.tensor.transpose(ot[:, tt, :], live["oT%d%d" % (hf, ht)][:, P * tt:P * (tt + 1)], ident_f[:])
+
+        def o_c(hf, ht):
+            cols = slice(P * ht, P * (ht + 1))
+            rows = slice(4 * hf, 4 * hf + 4)
+            copy_engine("oC%d%d" % (hf, ht))(out=osb[:, rows, cols], in_=live["ot%d%d" % (hf, ht)][:])
+            nc.sync.dma_start(out=outv[:, rows, cols], in_=osb[:, rows, cols])
+
+        two = {"wR": w_regroup, "wQ": w_quant, "xT": x_t, "xC": x_c, "xQ": x_q, "ab": ab, "at": at, "ns": ns,
+               "nT": n_t, "cT": c_t, "oT": o_t, "oR": o_tr, "oC": o_c}
+        for label in ORDER:
+            if label == "vecT":
+                vec_t()
+            elif label == "vec":
+                vec_v()
+            elif label == "rmax":
+                rmax()
+            elif label == "sens":
+                sens()
+            elif label == "mk":
+                mk_v()
+            elif label[0:3] == "red":
+                red(int(label[3]))
+            elif label[0:3] == "add":
+                add(int(label[4]), int(label[6]) // 2)
+            elif label[0] == "m":
+                mx(int(label[1]), int(label[2]), int(label[3]))
+            else:
+                two[label[0:2]](int(label[2]), int(label[3]))

@@ -18,21 +18,22 @@ FLOPS = 2 * 2 * B * F * H
 INV_EPS = 7.5
 P_KEEP = 0.95
 
-ON_VECTOR = ('xC04','at00','at01','at02','at03','at12',)
+ON_VECTOR = ('xC04','xC07','xC11','xC13','xC17','at00','at02','oC02','at03',)
 W2_ENGINE = ('V','V')
 ADD_ENGINE = {'adds1_23':'V'}
+NS_GROUPS = (('0123',),('01','23',),)
 ORDER = (
-    "wR00", "xT00", "vecT", "xT01", "xC00", "vec", "xC01", "wR01", "xT02", "wQ01", "xT03", "xC02",
-    "wQ00", "xC03", "xT04", "xQ02", "xT05", "xQ01", "xC04", "xC05", "xT06", "xQ00", "xT07", "xQ03",
-    "xC06", "m000", "xQ04", "xC07", "xQ06", "m001", "xQ05", "xQ07", "m003", "ab01", "at01", "m002",
-    "ab00", "at00", "m011", "ab03", "at03", "adds0_01", "m012", "at02", "ab02", "m013", "wR10",
-    "adds0_23", "m010", "ab12", "xT11", "ab11", "wQ10", "ns00", "ab10", "at12", "ab13", "adds1_01",
-    "xT10", "wR11", "ns01", "xC11", "xC10", "xQ11", "ns10", "adds1_23", "at10", "xQ10", "red0", "ns11",
-    "wQ11", "xT13", "red1", "xC13", "rmax", "sens", "at13", "nT00", "mk", "xQ13", "xT12", "cT00",
-    "nT01", "xC12", "cT01", "xT14", "xT15", "xC14", "xQ12", "nT10", "cT03", "xC15", "m101", "cT02",
-    "at11", "m100", "oT01", "xT17", "oT00", "xT16", "xC17", "m102", "xQ14", "xC16", "cT10", "m103",
-    "xQ17", "nT11", "xQ16", "xQ15", "oR00", "oT03", "oR01", "oC00", "oT02", "m110", "oC01", "cT11",
-    "oR02", "oT10", "oR03", "oC02", "m111", "cT12", "oC03", "oR10", "oT11", "m112", "oC10", "cT13",
+    "vecT", "wR00", "xT01", "vec", "wQ00", "xT00", "wR01", "xC00", "xT02", "xC01", "xT03", "xC02",
+    "xT05", "xQ01", "xQ00", "xC03", "xT04", "wQ01", "xC05", "xT06", "xQ02", "xQ03", "m000", "xC04",
+    "xC06", "m001", "xQ05", "xQ04", "ab00", "m002", "at00", "ab01", "xT07", "xQ06", "at02", "ab02",
+    "xT11", "adds0_01", "xC07", "at01", "m003", "xQ07", "m010", "adds0_012", "ab03", "at03", "m011",
+    "xC11", "ab10", "m012", "adds0_0123", "wR11", "ab11", "m013", "xT10", "ab12", "wR10", "adds1_01",
+    "xT13", "ab13", "ns00", "wQ11", "at12", "adds1_23", "at13", "ns10", "xC13", "xC10", "red0", "ns11",
+    "at10", "xQ13", "xQ10", "xT12", "red1", "xT15", "rmax", "xC12", "xQ11", "wQ10", "sens", "xC15",
+    "nT00", "xQ12", "xT17", "mk", "cT01", "xT14", "cT00", "nT01", "xC14", "xC17", "m101", "at11",
+    "cT02", "m100", "oT01", "nT10", "cT03", "xT16", "oT00", "oR01", "cT11", "xC16", "m102", "cT10",
+    "oR00", "xQ14", "nT11", "xQ16", "oT02", "oC00", "m103", "xQ17", "oC01", "xQ15", "m110", "oT03",
+    "oR02", "oT10", "oR03", "oC02", "m111", "cT12", "oC03", "oR10", "oT11", "m112", "cT13", "oC10",
     "oR11", "oT12", "m113", "oC11", "oR12", "oT13", "oC12", "oR13", "oC13",
 )
 
@@ -66,9 +67,9 @@ def tile_splitnn_pa_kernel(tc, x1, x2, W1, b1, W2, b2, noise_std, rr_uniform, ou
         warm2 = const.tile([P, 1], F32)
         nc.scalar.activation(out=warm2[:], in_=warm[:], func=ACT.Abs)
 
-        nc.scalar.dma_start(out=vraw[0:4, :], in_=b1.rearrange("(r c) -> r c", c=P))
-        nc.scalar.dma_start(out=vraw[4:8, :], in_=b2.rearrange("(r c) -> r c", c=P))
-        nc.scalar.dma_start(out=vraw[8:12, :], in_=rr_uniform.rearrange("(r c) -> r c", c=P))
+        nc.sync.dma_start(out=vraw[0:4, :], in_=b1.rearrange("(r c) -> r c", c=P))
+        nc.sync.dma_start(out=vraw[4:8, :], in_=b2.rearrange("(r c) -> r c", c=P))
+        nc.sync.dma_start(out=vraw[8:12, :], in_=rr_uniform.rearrange("(r c) -> r c", c=P))
 
         wraw = [const.tile([P, 2, 4, H], BF16, name="wraw%d" % c) for c in range(2)]
         xraw = [const.tile([P, 8 * F], BF16, name="xraw%d" % c) for c in range(2)]
@@ -199,18 +200,21 @@ def tile_splitnn_pa_kernel(tc, x1, x2, W1, b1, W2, b2, noise_std, rr_uniform, ou
                 nc.scalar.activation(out=dst, in_=src, func=ACT.Identity, bias=b1k[:, ht:ht + 1],
                                      scale=keep[:, ht:ht + 1])
 
-        def add(hf, pair):
+        def add(label):
+            hf = int(label[4])
+            hts = label[6:]
             t = sump.tile([P, 512], F32, tag="s")
-            live["s%d%d" % (hf, pair)] = t
-            eng = nc.vector if ADD_ENGINE.get("adds%d_%d%d" % (hf, 2 * pair, 2 * pair + 1), "G") == "V" else nc.gpsimd
-            eng.tensor_tensor(out=t[:], in0=live["ab%d%d" % (hf, 2 * pair)][:],
-                              in1=live["ab%d%d" % (hf, 2 * pair + 1)][:], op=ALU.add)
+            first = live["ab%d%s" % (hf, hts[0])] if len(hts) == 2 else live["s%d_%s" % (hf, hts[0:len(hts) - 1])]
+            live["s%d_%s" % (hf, hts)] = t
+            eng = nc.vector if ADD_ENGINE.get(label, "G") == "V" else nc.gpsimd
+            eng.tensor_tensor(out=t[:], in0=first[:], in1=live["ab%d%s" % (hf, hts[len(hts) - 1])][:], op=ALU.add)
 
-        def ns(hf, pair):
-            if pair == 0:
+        def ns(hf, gi):
+            groups = NS_GROUPS[hf]
+            if gi == 0:
                 live["ns%d" % hf] = psum.tile([P, 512], F32, tag="nz", name="ns")
-            nc.tensor.matmul(out=live["ns%d" % hf][:], lhsT=plusminus[:], rhs=live["s%d%d" % (hf, pair)][:],
-                             start=(pair == 0), stop=(pair == 1))
+            nc.tensor.matmul(out=live["ns%d" % hf][:], lhsT=plusminus[:], rhs=live["s%d_%s" % (hf, groups[gi])][:],
+                             start=(gi == 0), stop=(gi == len(groups) - 1))
 
         def red(hf):
             nc.vector.tensor_reduce(out=r2[:, hf:hf + 1], in_=live["ns%d" % hf][:], axis=AX.X, op=ALU.max)
@@ -276,7 +280,7 @@ def tile_splitnn_pa_kernel(tc, x1, x2, W1, b1, W2, b2, noise_std, rr_uniform, ou
             elif label[0:3] == "red":
                 red(int(label[3]))
             elif label[0:3] == "add":
-                add(int(label[4]), int(label[6]) // 2)
+                add(label)
             elif label[0] == "m":
                 mx(int(label[1]), int(label[2]), int(label[3]))
             else:

@@ -18,23 +18,23 @@ FLOPS = 2 * 2 * B * F * H
 INV_EPS = 7.5
 P_KEEP = 0.95
 
-ON_VECTOR = ('xC04','xC07','xC11','xC13','xC17','at00','at02','oC02','at03',)
+ON_VECTOR = ('xC04','xC07','xC11','xC15','oC00','at03',)
 W2_ENGINE = ('V','V')
-ADD_ENGINE = {'adds1_23':'V'}
+ADD_ENGINE = {'adds0_01':'V','adds0_012':'V','adds0_0123':'V','adds1_01':'V','adds1_23':'V'}
 NS_GROUPS = (('0123',),('01','23',),)
 ORDER = (
-    "vecT", "wR00", "xT01", "vec", "wQ00", "xT00", "wR01", "xC00", "xT02", "xC01", "xT03", "xC02",
-    "xT05", "xQ01", "xQ00", "xC03", "xT04", "wQ01", "xC05", "xT06", "xQ02", "xQ03", "m000", "xC04",
-    "xC06", "m001", "xQ05", "xQ04", "ab00", "m002", "at00", "ab01", "xT07", "xQ06", "at02", "ab02",
-    "xT11", "adds0_01", "xC07", "at01", "m003", "xQ07", "m010", "adds0_012", "ab03", "at03", "m011",
-    "xC11", "ab10", "m012", "adds0_0123", "wR11", "ab11", "m013", "xT10", "ab12", "wR10", "adds1_01",
-    "xT13", "ab13", "ns00", "wQ11", "at12", "adds1_23", "at13", "ns10", "xC13", "xC10", "red0", "ns11",
-    "at10", "xQ13", "xQ10", "xT12", "red1", "xT15", "rmax", "xC12", "xQ11", "wQ10", "sens", "xC15",
-    "nT00", "xQ12", "xT17", "mk", "cT01", "xT14", "cT00", "nT01", "xC14", "xC17", "m101", "at11",
-    "cT02", "m100", "oT01", "nT10", "cT03", "xT16", "oT00", "oR01", "cT11", "xC16", "m102", "cT10",
-    "oR00", "xQ14", "nT11", "xQ16", "oT02", "oC00", "m103", "xQ17", "oC01", "xQ15", "m110", "oT03",
-    "oR02", "oT10", "oR03", "oC02", "m111", "cT12", "oC03", "oR10", "oT11", "m112", "cT13", "oC10",
-    "oR11", "oT12", "m113", "oC11", "oR12", "oT13", "oC12", "oR13", "oC13",
+    "vecT", "wR00", "xT01", "vec", "xT00", "wR01", "xC01", "xC00", "xT02", "wQ00", "xT03", "wQ01",
+    "xC02", "xT05", "xQ01", "xQ00", "xC03", "xT04", "xQ02", "xC05", "xT06", "xQ03", "m000", "xC04",
+    "xC06", "m001", "xQ05", "xQ04", "ab00", "m003", "xQ06", "ab01", "xT07", "wR11", "at01", "m002",
+    "xC07", "at00", "xT11", "xQ07", "at02", "adds0_01", "m011", "ab02", "at03", "m012", "xC11", "ab03",
+    "xT13", "adds0_012", "ab11", "m010", "adds0_0123", "ab12", "xT10", "wR10", "ab10", "m013", "xC10",
+    "ns00", "adds1_01", "ab13", "wQ10", "xT12", "xC13", "adds1_23", "ns10", "xC12", "wQ11", "at11",
+    "ns11", "xQ10", "red0", "at10", "xT15", "at12", "red1", "rmax", "xC15", "sens", "xQ11", "nT00",
+    "xQ12", "mk", "xT17", "xQ13", "cT01", "nT01", "xC17", "cT00", "xT14", "at13", "cT02", "m101",
+    "xQ15", "xT16", "xQ17", "oT01", "nT10", "cT03", "xC16", "m100", "xC14", "cT10", "oR01", "oT00",
+    "m103", "xQ16", "oC01", "nT11", "xQ14", "cT11", "m102", "oT03", "oR00", "oT02", "m110", "oC00",
+    "oR03", "cT12", "oR02", "oT10", "oC03", "m111", "cT13", "oC02", "oR10", "oT11", "m112", "oC10",
+    "m113", "oT12", "oR11", "oT13", "oR12", "oC11", "oC12", "oR13", "oC13",
 )
 
 
@@ -43,9 +43,9 @@ def tile_splitnn_pa_kernel(tc, x1, x2, W1, b1, W2, b2, noise_std, rr_uniform, ou
     with ExitStack() as ctx:
         ctx.enter_context(tc.manual_schedule())
         const = ctx.enter_context(tc.tile_pool(name="const", bufs=1))
-        stage = ctx.enter_context(tc.tile_pool(name="stage", bufs=4))
-        absp = ctx.enter_context(tc.tile_pool(name="absp", bufs=4))
-        sump = ctx.enter_context(tc.tile_pool(name="sump", bufs=3))
+        stage = ctx.enter_context(tc.tile_pool(name="stage", bufs=6))
+        absp = ctx.enter_context(tc.tile_pool(name="absp", bufs=8))
+        sump = ctx.enter_context(tc.tile_pool(name="sump", bufs=4))
         outp = ctx.enter_context(tc.tile_pool(name="outp", bufs=8))
         psum = ctx.enter_context(tc.psum_pool(name="psum", bufs=2))
 

@@ -18,23 +18,23 @@ FLOPS = 2 * 2 * B * F * H
 INV_EPS = 7.5
 P_KEEP = 0.95
 
-ON_VECTOR = ('xC04','xC07','xC11','xC15','oC00','at03',)
+ON_VECTOR = ('xC07','xC10','xC11','xC13','oC12',)
 W2_ENGINE = ('V','V')
 ADD_ENGINE = {'adds0_01':'V','adds0_012':'V','adds0_0123':'V','adds1_01':'V','adds1_23':'V'}
 NS_GROUPS = (('0123',),('01','23',),)
 ORDER = (
-    "vecT", "wR00", "xT01", "vec", "xT00", "wR01", "xC01", "xC00", "xT02", "wQ00", "xT03", "wQ01",
-    "xC02", "xT05", "xQ01", "xQ00", "xC03", "xT04", "xQ02", "xC05", "xT06", "xQ03", "m000", "xC04",
-    "xC06", "m001", "xQ05", "xQ04", "ab00", "m003", "xQ06", "ab01", "xT07", "wR11", "at01", "m002",
-    "xC07", "at00", "xT11", "xQ07", "at02", "adds0_01", "m011", "ab02", "at03", "m012", "xC11", "ab03",
-    "xT13", "adds0_012", "ab11", "m010", "adds0_0123", "ab12", "xT10", "wR10", "ab10", "m013", "xC10",
-    "ns00", "adds1_01", "ab13", "wQ10", "xT12", "xC13", "adds1_23", "ns10", "xC12", "wQ11", "at11",
-    "ns11", "xQ10", "red0", "at10", "xT15", "at12", "red1", "rmax", "xC15", "sens", "xQ11", "nT00",
-    "xQ12", "mk", "xT17", "xQ13", "cT01", "nT01", "xC17", "cT00", "xT14", "at13", "cT02", "m101",
-    "xQ15", "xT16", "xQ17", "oT01", "nT10", "cT03", "xC16", "m100", "xC14", "cT10", "oR01", "oT00",
-    "m103", "xQ16", "oC01", "nT11", "xQ14", "cT11", "m102", "oT03", "oR00", "oT02", "m110", "oC00",
-    "oR03", "cT12", "oR02", "oT10", "oC03", "m111", "cT13", "oC02", "oR10", "oT11", "m112", "oC10",
-    "m113", "oT12", "oR11", "oT13", "oR12", "oC11", "oC12", "oR13", "oC13",
+    "wR00", "xT01", "wQ00", "xT00", "wR01", "xC01", "vecT", "xC00", "xT02", "xT03", "xQ00", "xQ01",
+    "xC02", "xT04", "vec", "wQ01", "xC03", "xT05", "xQ02", "xC04", "xT06", "xQ03", "xC05", "m001",
+    "xQ04", "xC06", "m000", "xQ05", "ab01", "m002", "xQ06", "ab00", "xT07", "wR11", "ab02", "m003",
+    "xC07", "at02", "xT10", "xQ07", "at01", "adds0_01", "m011", "at03", "wR10", "m010", "ab03", "m013",
+    "adds0_012", "m012", "at00", "xC10", "xT11", "ab10", "adds0_0123", "xT12", "ab11", "xC11", "xT13",
+    "ab13", "ns00", "adds1_01", "ab12", "at13", "ns10", "adds1_23", "xC12", "xC13", "ns11", "xQ10",
+    "xQ11", "xQ13", "red0", "xT14", "red1", "xT15", "rmax", "xC14", "xT16", "xQ12", "wQ10", "at10",
+    "sens", "nT00", "wQ11", "at11", "nT11", "xQ14", "mk", "cT01", "at12", "nT01", "cT00", "xT17",
+    "cT03", "m101", "xC17", "cT12", "m100", "xC16", "oT01", "m103", "xC15", "oT00", "nT10", "cT02",
+    "oR00", "xQ17", "xQ15", "m102", "cT10", "oR01", "xQ16", "oT03", "m110", "oT02", "oC01", "oR03",
+    "cT11", "oC00", "oR02", "cT13", "oC03", "m111", "oT10", "oC02", "m112", "oT11", "oR10", "oT12",
+    "m113", "oC10", "oR11", "oT13", "oR12", "oC11", "oR13", "oC12", "oC13",
 )
 
 
@@ -47,7 +47,7 @@ def tile_splitnn_pa_kernel(tc, x1, x2, W1, b1, W2, b2, noise_std, rr_uniform, ou
         absp = ctx.enter_context(tc.tile_pool(name="absp", bufs=8))
         sump = ctx.enter_context(tc.tile_pool(name="sump", bufs=4))
         outp = ctx.enter_context(tc.tile_pool(name="outp", bufs=8))
-        psum = ctx.enter_context(tc.psum_pool(name="psum", bufs=2))
+        psum = ctx.enter_context(tc.psum_pool(name="psum", bufs=8))
 
         ident_f = const.tile([P, P], F32)
         make_identity(nc, ident_f[:])
@@ -117,7 +117,7 @@ def tile_splitnn_pa_kernel(tc, x1, x2, W1, b1, W2, b2, noise_std, rr_uniform, ou
             return nc.vector.tensor_copy if label in ON_VECTOR else nc.scalar.copy
 
         def vec_t():
-            vps = psum.tile([P, P], BF16, tag="nz")
+            vps = psum.tile([P, P], BF16, tag="ps")
             live["vps"] = vps
             nc.tensor.transpose(vps[:], vraw[:], ident_b[:])
 
@@ -147,7 +147,7 @@ def tile_splitnn_pa_kernel(tc, x1, x2, W1, b1, W2, b2, noise_std, rr_uniform, ou
         def x_t(c, i):
             j, g = i // 2, i % 2
             xw = xraw[c][:].bitcast(F32)
-            xt = psum.tile([P, 2, 2, P], F32, tag=("nz" if (c == 0 and i % 4 >= 2) else "xt"))
+            xt = psum.tile([P, 2, 2, P], F32, tag="ps")
             live["xt%d%d" % (c, i)] = xt
             for tt in range(2):
                 for u in range(2):
@@ -172,7 +172,7 @@ def tile_splitnn_pa_kernel(tc, x1, x2, W1, b1, W2, b2, noise_std, rr_uniform, ou
             )
 
         def mx(c, hf, ht):
-            acc = psum.tile([P, 512], F32, tag=("ot" if (c == 0 and ht % 2 == 1) else "acc"))
+            acc = psum.tile([P, 512], F32, tag="ps")
             live["acc%d%d%d" % (c, hf, ht)] = acc
             for g in range(2):
                 nc.tensor.matmul_mx(
@@ -212,7 +212,7 @@ def tile_splitnn_pa_kernel(tc, x1, x2, W1, b1, W2, b2, noise_std, rr_uniform, ou
         def ns(hf, gi):
             groups = NS_GROUPS[hf]
             if gi == 0:
-                live["ns%d" % hf] = psum.tile([P, 512], F32, tag="nz", name="ns")
+                live["ns%d" % hf] = psum.tile([P, 512], F32, tag="ps", name="ns")
             nc.tensor.matmul(out=live["ns%d" % hf][:], lhsT=plusminus[:], rhs=live["s%d_%s" % (hf, groups[gi])][:],
                              start=(gi == 0), stop=(gi == len(groups) - 1))
 
@@ -224,7 +224,7 @@ def tile_splitnn_pa_kernel(tc, x1, x2, W1, b1, W2, b2, noise_std, rr_uniform, ou
                                     in1=r2[:, 1:2].to_broadcast([P, 2]), op=ALU.max)
 
         def sens():
-            live["sens"] = psum.tile([P, 2], F32, tag="nz", name="sens")
+            live["sens"] = psum.tile([P, 2], F32, tag="ps", name="sens")
             nc.tensor.matmul(out=live["sens"][:], lhsT=pick[:], rhs=rr2[:], start=True, stop=True)
 
         def mk_v():
@@ -232,7 +232,7 @@ def tile_splitnn_pa_kernel(tc, x1, x2, W1, b1, W2, b2, noise_std, rr_uniform, ou
                                     op=ALU.mult)
 
         def n_t(hf, hp):
-            nz = psum.tile([P, 2, 512], BF16, tag="nz")
+            nz = psum.tile([P, 2, 512], BF16, tag="ps")
             live["nz%d%d" % (hf, hp)] = nz
             for a in range(2):
                 ht = 2 * hp + a
@@ -253,7 +253,7 @@ def tile_splitnn_pa_kernel(tc, x1, x2, W1, b1, W2, b2, noise_std, rr_uniform, ou
                                            in1=a_t[:, ht, 512 * hf:512 * (hf + 1)], op0=ALU.add, op1=ALU.min)
 
         def o_tr(hf, ht):
-            ot = psum.tile([P, 4, P], F32, tag="ot")
+            ot = psum.tile([P, 4, P], F32, tag="ps")
             live["ot%d%d" % (hf, ht)] = ot
             for tt in range(4):
                 nc.tensor.transpose(ot[:, tt, :], live["oT%d%d" % (hf, ht)][:, P * tt:P * (tt + 1)], ident_f[:])

@@ -18,23 +18,23 @@ FLOPS = 2 * 2 * B * F * H
 INV_EPS = 7.5
 P_KEEP = 0.95
 
-ON_VECTOR = ('xC07','xC10','xC11','xC13','oC12',)
+ON_VECTOR = ('xC00','xC03','xC07','xC11','at00','at02',)
 W2_ENGINE = ('V','V')
 ADD_ENGINE = {'adds0_01':'V','adds0_012':'V','adds0_0123':'V','adds1_01':'V','adds1_23':'V'}
 NS_GROUPS = (('0123',),('01','23',),)
 ORDER = (
-    "wR00", "xT01", "wQ00", "xT00", "wR01", "xC01", "vecT", "xC00", "xT02", "xT03", "xQ00", "xQ01",
-    "xC02", "xT04", "vec", "wQ01", "xC03", "xT05", "xQ02", "xC04", "xT06", "xQ03", "xC05", "m001",
-    "xQ04", "xC06", "m000", "xQ05", "ab01", "m002", "xQ06", "ab00", "xT07", "wR11", "ab02", "m003",
-    "xC07", "at02", "xT10", "xQ07", "at01", "adds0_01", "m011", "at03", "wR10", "m010", "ab03", "m013",
-    "adds0_012", "m012", "at00", "xC10", "xT11", "ab10", "adds0_0123", "xT12", "ab11", "xC11", "xT13",
-    "ab13", "ns00", "adds1_01", "ab12", "at13", "ns10", "adds1_23", "xC12", "xC13", "ns11", "xQ10",
-    "xQ11", "xQ13", "red0", "xT14", "red1", "xT15", "rmax", "xC14", "xT16", "xQ12", "wQ10", "at10",
-    "sens", "nT00", "wQ11", "at11", "nT11", "xQ14", "mk", "cT01", "at12", "nT01", "cT00", "xT17",
-    "cT03", "m101", "xC17", "cT12", "m100", "xC16", "oT01", "m103", "xC15", "oT00", "nT10", "cT02",
-    "oR00", "xQ17", "xQ15", "m102", "cT10", "oR01", "xQ16", "oT03", "m110", "oT02", "oC01", "oR03",
-    "cT11", "oC00", "oR02", "cT13", "oC03", "m111", "oT10", "oC02", "m112", "oT11", "oR10", "oT12",
-    "m113", "oC10", "oR11", "oT13", "oR12", "oC11", "oR13", "oC12", "oC13",
+    "wR00", "xT00", "wQ00", "xT01", "xC00", "xC01", "xQ00", "wR01", "xT02", "vecT", "xT03", "wQ01",
+    "xC02", "xT05", "xQ01", "xT04", "xC03", "xC05", "xQ02", "xT06", "xQ03", "xC04", "m001", "vec",
+    "xQ05", "xC06", "xT07", "xQ04", "m000", "at01", "xC07", "m002", "ab01", "xQ07", "m003", "at00",
+    "ab00", "xT10", "xQ06", "ab02", "at02", "xT11", "ab03", "m012", "adds0_01", "xC10", "m010", "xC11",
+    "at03", "adds0_012", "xT14", "ab10", "m011", "xQ11", "xQ10", "xC14", "adds0_0123", "xT13", "m013",
+    "ab11", "wR11", "ns00", "ab12", "adds1_01", "ab13", "xT12", "wQ11", "xC13", "ns10", "adds1_23",
+    "at11", "xQ14", "at13", "wR10", "ns11", "at10", "red0", "xC12", "xT15", "xT17", "red1", "xT16",
+    "rmax", "xQ13", "xQ12", "xC16", "sens", "wQ10", "nT00", "at12", "nT01", "mk", "xQ16", "xC15",
+    "m102", "cT01", "xC17", "cT00", "m100", "m101", "xQ15", "cT03", "nT10", "xQ17", "m103", "oT01",
+    "cT11", "nT11", "oT00", "m110", "cT02", "oR01", "oR00", "oT02", "m111", "oT03", "oC00", "oR02",
+    "cT10", "oC01", "oR03", "cT13", "m113", "oC02", "oT10", "oC03", "m112", "oT11", "oR10", "cT12",
+    "oR11", "oT12", "oC10", "oT13", "oC11", "oR12", "oR13", "oC12", "oC13",
 )
 
 

@@ -15,31 +15,45 @@ AX = mybir.AxisListType
 P = 128
 B, F, H = 1024, 1024, 512
 FLOPS = 2 * 2 * B * F * H
+TILES = B // P
+PASSES = F // (4 * P)
+H_TILES = H // P
+HALF = 512
 INV_EPS = 7.5
 P_KEEP = 0.95
 
-ON_VECTOR = ('xC00','xC03','xC07','xC11','at00','at02',)
-W2_ENGINE = ('V','V')
-ADD_ENGINE = {'adds0_01':'V','adds0_012':'V','adds0_0123':'V','adds1_01':'V','adds1_23':'V'}
-NS_GROUPS = (('0123',),('01','23',),)
-ORDER = (
-    "wR00", "xT00", "wQ00", "xT01", "xC00", "xC01", "xQ00", "wR01", "xT02", "vecT", "xT03", "wQ01",
-    "xC02", "xT05", "xQ01", "xT04", "xC03", "xC05", "xQ02", "xT06", "xQ03", "xC04", "m001", "vec",
-    "xQ05", "xC06", "xT07", "xQ04", "m000", "at01", "xC07", "m002", "ab01", "xQ07", "m003", "at00",
-    "ab00", "xT10", "xQ06", "ab02", "at02", "xT11", "ab03", "m012", "adds0_01", "xC10", "m010", "xC11",
-    "at03", "adds0_012", "xT14", "ab10", "m011", "xQ11", "xQ10", "xC14", "adds0_0123", "xT13", "m013",
-    "ab11", "wR11", "ns00", "ab12", "adds1_01", "ab13", "xT12", "wQ11", "xC13", "ns10", "adds1_23",
-    "at11", "xQ14", "at13", "wR10", "ns11", "at10", "red0", "xC12", "xT15", "xT17", "red1", "xT16",
-    "rmax", "xQ13", "xQ12", "xC16", "sens", "wQ10", "nT00", "at12", "nT01", "mk", "xQ16", "xC15",
-    "m102", "cT01", "xC17", "cT00", "m100", "m101", "xQ15", "cT03", "nT10", "xQ17", "m103", "oT01",
-    "cT11", "nT11", "oT00", "m110", "cT02", "oR01", "oR00", "oT02", "m111", "oT03", "oC00", "oR02",
-    "cT10", "oC01", "oR03", "cT13", "m113", "oC02", "oT10", "oC03", "m112", "oT11", "oR10", "cT12",
-    "oR11", "oT12", "oC10", "oT13", "oC11", "oR12", "oR13", "oC12", "oC13",
-)
+
+def names(prefix, first, last):
+    return [prefix + str(i) for i in range(first, last + 1)]
+
+
+def engine_queues():
+    tensor = (
+        ["xt00", "xt01", "vt"] + names("xt0", 2, 6) + names("mm00", 0, 2) + ["xt07", "mm003", "xt10"]
+        + names("mm01", 0, 3) + names("xt1", 1, 3) + ["ns00", "ns10", "ns11"] + names("xt1", 4, 6)
+        + ["se", "nt00", "nt01", "nt10", "xt17"] + names("mm10", 0, 2)
+        + ["nt11", "tr00", "mm103", "tr01", "mm110", "tr02", "tr03", "mm111", "mm112", "tr10", "mm113"]
+        + names("tr1", 1, 3)
+    )
+    vector = (
+        ["wr00", "wq00", "wr01", "xq00", "xq01", "vv", "wq01"] + names("xq0", 2, 6)
+        + ["wr10", "xc07", "xq07", "su00", "wr11", "su01", "xc10", "su02", "xc11", "su10", "su11", "xc13"]
+        + ["xq10", "xq11", "xq13", "rd0", "rd1", "rm", "xq12", "wq10", "wq11", "xq14", "mk"]
+        + ["ct00", "ct01", "ct02", "ct10", "mn00", "mn01", "ct03", "xq15", "xq17", "ct11", "xq16", "mn02", "mn03"]
+        + ["ct12", "ct13"] + names("mn1", 0, 3) + ["oc12"]
+    )
+    scalar = (
+        names("xc0", 0, 6) + ["ab00", "ab01", "ab02", "am00", "am01", "am02", "ab03", "am03"] + names("ab1", 0, 3)
+        + ["am13", "xc12", "xc14", "am10", "am11", "am12", "xc15", "xc16", "xc17"] + names("oc0", 0, 3)
+        + ["oc10", "oc11", "oc13"]
+    )
+    sync = names("st0", 0, 3) + names("st1", 0, 3)
+    return tensor, vector, scalar, sync
 
 
 def tile_splitnn_pa_kernel(tc, x1, x2, W1, b1, W2, b2, noise_std, rr_uniform, out):
     nc = tc.nc
+    tensor_queue, vector_queue, scalar_queue, sync_queue = engine_queues()
     with ExitStack() as ctx:
         ctx.enter_context(tc.manual_schedule())
         const = ctx.enter_context(tc.tile_pool(name="const", bufs=1))
@@ -53,37 +67,37 @@ def tile_splitnn_pa_kernel(tc, x1, x2, W1, b1, W2, b2, noise_std, rr_uniform, ou
         make_identity(nc, ident_f[:])
         ident_b = const.tile([P, P], BF16)
         make_identity(nc, ident_b[:])
-        vraw = const.tile([P, P], BF16)
-        nc.vector.memset(vraw[:], 0.0)
-        plusminus = const.tile([P, P], F32)
-        nc.vector.memset(plusminus[:, 0:64], 1.0)
-        nc.vector.memset(plusminus[:, 64:128], -1.0)
+        vec_rows = const.tile([P, P], BF16)
+        nc.vector.memset(vec_rows[:], 0.0)
+        plus_minus = const.tile([P, P], F32)
+        nc.vector.memset(plus_minus[:, 0:64], 1.0)
+        nc.vector.memset(plus_minus[:, 64:128], -1.0)
         pick = const.tile([P, P], F32)
         nc.vector.memset(pick[:], 0.0)
         nc.vector.memset(pick[0:1, :], 1.0)
         nc.vector.memset(pick[64:65, :], 1.0)
-        warm = const.tile([P, 1], F32)
-        nc.vector.memset(warm[:], 0.0)
-        warm2 = const.tile([P, 1], F32)
-        nc.scalar.activation(out=warm2[:], in_=warm[:], func=ACT.Abs)
+        zero_col = const.tile([P, 1], F32)
+        nc.vector.memset(zero_col[:], 0.0)
+        table_warm = const.tile([P, 1], F32)
+        nc.scalar.activation(out=table_warm[:], in_=zero_col[:], func=ACT.Abs)
 
-        nc.sync.dma_start(out=vraw[0:4, :], in_=b1.rearrange("(r c) -> r c", c=P))
-        nc.sync.dma_start(out=vraw[4:8, :], in_=b2.rearrange("(r c) -> r c", c=P))
-        nc.sync.dma_start(out=vraw[8:12, :], in_=rr_uniform.rearrange("(r c) -> r c", c=P))
+        nc.sync.dma_start(out=vec_rows[0:4, :], in_=b1.rearrange("(r c) -> r c", c=P))
+        nc.sync.dma_start(out=vec_rows[4:8, :], in_=b2.rearrange("(r c) -> r c", c=P))
+        nc.sync.dma_start(out=vec_rows[8:12, :], in_=rr_uniform.rearrange("(r c) -> r c", c=P))
 
-        wraw = [const.tile([P, 2, 4, H], BF16, name="wraw%d" % c) for c in range(2)]
-        xraw = [const.tile([P, 8 * F], BF16, name="xraw%d" % c) for c in range(2)]
-        nraw = const.tile([P, 8, H], BF16)
+        w_raw = [const.tile([P, PASSES, 4, H], BF16, name="w_raw%d" % c) for c in range(2)]
+        x_raw = [const.tile([P, TILES * F], BF16, name="x_raw%d" % c) for c in range(2)]
+        noise = const.tile([P, TILES, H], BF16)
 
-        def load_w(c, W, g):
+        def load_w(c, w, g):
             nc.sync.dma_start(
-                out=wraw[c][:, g].rearrange("q (u e) h -> q u (e h)", u=2),
-                in_=W[512 * g:512 * (g + 1), :].rearrange("(u q e) h -> q u (e h)", u=2, e=2),
+                out=w_raw[c][:, g].rearrange("q (u e) h -> q u (e h)", u=2),
+                in_=w[512 * g:512 * (g + 1), :].rearrange("(u q e) h -> q u (e h)", u=2, e=2),
             )
 
         def load_x(c, x, j):
-            xv = x.rearrange("(p t) k -> p (t k)", t=8)
-            nc.sync.dma_start(out=xraw[c][:, 2048 * j:2048 * (j + 1)], in_=xv[:, 2048 * j:2048 * (j + 1)])
+            cols = slice(2 * F * j, 2 * F * (j + 1))
+            nc.sync.dma_start(out=x_raw[c][:, cols], in_=x.rearrange("(p t) k -> p (t k)", t=TILES)[:, cols])
 
         load_w(0, W1, 0)
         load_x(0, x1, 0)
@@ -94,194 +108,212 @@ def tile_splitnn_pa_kernel(tc, x1, x2, W1, b1, W2, b2, noise_std, rr_uniform, ou
         load_w(1, W2, 1)
         for j in range(4):
             load_x(1, x2, j)
-        nc.sync.dma_start(out=nraw[:], in_=noise_std.rearrange("(p t) h -> p t h", t=8))
+        nc.sync.dma_start(out=noise[:], in_=noise_std.rearrange("(p t) h -> p t h", t=TILES))
 
+        w_grouped = [const.tile([P, PASSES, H, 4], BF16, name="w_grouped%d" % c, align_bytes=64) for c in range(2)]
+        w_words = [const.tile([P, PASSES, H], U32, name="w_words%d" % c, align_bytes=64) for c in range(2)]
+        w_scales = [const.tile([P, PASSES, H], U8, name="w_scales%d" % c, align_bytes=64) for c in range(2)]
+        x_words = [const.tile([P, 2, PASSES, HALF], U32, name="x_words%d" % c, align_bytes=64) for c in range(2)]
+        x_scales = [const.tile([P, 2, PASSES, HALF], U8, name="x_scales%d" % c, align_bytes=64) for c in range(2)]
         vec = const.tile([P, 12], F32)
-        keep = const.tile([P, 4], F32)
-        b1k = const.tile([P, 4], F32)
-        keep_e = const.tile([P, 4], F32)
-        wgrp = [const.tile([P, 2, H, 4], BF16, name="wgrp%d" % c, align_bytes=64) for c in range(2)]
-        wq = [const.tile([P, 2, H], U32, name="wq%d" % c, align_bytes=64) for c in range(2)]
-        ws = [const.tile([P, 2, H], U8, name="ws%d" % c, align_bytes=64) for c in range(2)]
-        xq = [const.tile([P, 2, 2, 512], U32, name="xq%d" % c, align_bytes=64) for c in range(2)]
-        xs = [const.tile([P, 2, 2, 512], U8, name="xs%d" % c, align_bytes=64) for c in range(2)]
-        a_t = const.tile([P, 4, B], F32)
-        r2 = const.tile([P, 2], F32)
-        rr2 = const.tile([P, 2], F32)
-        mk = const.tile([P, 4], F32)
-        osb = const.tile([P, 8, H], F32)
-        outv = out.rearrange("(p t) h -> p t h", t=8)
+        keep = const.tile([P, H_TILES], F32)
+        b1_kept = const.tile([P, H_TILES], F32)
+        keep_over_eps = const.tile([P, H_TILES], F32)
+        noise_scale = const.tile([P, H_TILES], F32)
+        c_t = const.tile([P, H_TILES, B], F32)
+        half_max = const.tile([P, 2], F32)
+        both_max = const.tile([P, 2], F32)
+        out_rows = const.tile([P, TILES, H], F32)
+        out_view = out.rearrange("(p t) h -> p t h", t=TILES)
         live = {}
 
-        def copy_engine(label):
-            return nc.vector.tensor_copy if label in ON_VECTOR else nc.scalar.copy
+        def psum_copy(name):
+            return nc.vector.tensor_copy if name in vector_queue else nc.scalar.copy
 
-        def vec_t():
-            vps = psum.tile([P, P], BF16, tag="ps")
-            live["vps"] = vps
-            nc.tensor.transpose(vps[:], vraw[:], ident_b[:])
+        def vt():
+            live["vt"] = psum.tile([P, P], BF16, tag="bank", name="vec_t")
+            nc.tensor.transpose(live["vt"][:], vec_rows[:], ident_b[:])
 
-        def vec_v():
-            nc.vector.tensor_copy(out=vec[:], in_=live["vps"][:, 0:12])
+        def vv():
+            nc.vector.tensor_copy(out=vec[:], in_=live["vt"][:, 0:12])
             nc.vector.tensor_single_scalar(out=keep[:], in_=vec[:, 8:12], scalar=P_KEEP, op=ALU.is_lt)
-            nc.vector.tensor_tensor(out=b1k[:], in0=vec[:, 0:4], in1=keep[:], op=ALU.mult)
-            nc.vector.tensor_single_scalar(out=keep_e[:], in_=keep[:], scalar=INV_EPS, op=ALU.mult)
+            nc.vector.tensor_tensor(out=b1_kept[:], in0=vec[:, 0:4], in1=keep[:], op=ALU.mult)
+            nc.vector.tensor_single_scalar(out=keep_over_eps[:], in_=keep[:], scalar=INV_EPS, op=ALU.mult)
 
-        def w_regroup(c, g):
-            dst = wgrp[c][:, g].rearrange("p (c i) t -> p c t i", i=4)
-            src = wraw[c][:, g].rearrange("p t (c i) -> p c t i", i=4)
-            eng = W2_ENGINE[g] if c == 1 else "V"
-            if eng == "V":
-                nc.vector.tensor_copy(out=dst, in_=src)
-            elif eng == "S":
-                nc.scalar.copy(out=dst, in_=src)
-            else:
-                nc.gpsimd.tensor_scalar(out=dst, in0=src, scalar1=1.0, scalar2=0.0, op0=ALU.mult, op1=ALU.add)
-
-        def w_quant(c, g):
-            nc.vector.quantize_mx(
-                out=wq[c][:, g, :].bitcast(FP8X4), scales=ws[c][:, g, :],
-                in_=wgrp[c][:, g].rearrange("p h t -> p (h t)"),
+        def wr(c, g):
+            nc.vector.tensor_copy(
+                out=w_grouped[c][:, g].rearrange("p (c i) t -> p c t i", i=4),
+                in_=w_raw[c][:, g].rearrange("p t (c i) -> p c t i", i=4),
             )
 
-        def x_t(c, i):
+        def wq(c, g):
+            nc.vector.quantize_mx(
+                out=w_words[c][:, g, :].bitcast(FP8X4), scales=w_scales[c][:, g, :],
+                in_=w_grouped[c][:, g].rearrange("p h t -> p (h t)"),
+            )
+
+        def xt(c, i):
             j, g = i // 2, i % 2
-            xw = xraw[c][:].bitcast(F32)
-            xt = psum.tile([P, 2, 2, P], F32, tag="ps")
-            live["xt%d%d" % (c, i)] = xt
+            words = x_raw[c][:].bitcast(F32)
+            bank = psum.tile([P, 2, 2, P], F32, tag="bank", name="x_t")
+            live["xt%d%d" % (c, i)] = bank
             for tt in range(2):
                 for u in range(2):
-                    off = 512 * (2 * j + tt) + 256 * g + 128 * u
-                    nc.tensor.transpose(xt[:, tt, u, :], xw[:, off:off + P], ident_f[:])
+                    first = (F // 2) * (2 * j + tt) + 256 * g + P * u
+                    nc.tensor.transpose(bank[:, tt, u, :], words[:, first:first + P], ident_f[:])
 
-        def x_c(c, i):
-            stg = stage.tile([P, 1024], BF16, tag="stg", align_bytes=64)
-            live["stg%d%d" % (c, i)] = stg
-            copy_engine("xC%d%d" % (c, i))(
-                out=stg[:].bitcast(F32).rearrange("q (tt r u) -> q tt r u", tt=2, u=2),
+        def xc(c, i):
+            name = "xc%d%d" % (c, i)
+            grouped = stage.tile([P, 4 * 2 * P], BF16, tag="grouped", align_bytes=64)
+            live[name] = grouped
+            psum_copy(name)(
+                out=grouped[:].bitcast(F32).rearrange("q (tt r u) -> q tt r u", tt=2, u=2),
                 in_=live["xt%d%d" % (c, i)][:].rearrange("q tt u r -> q tt r u"),
             )
 
-        def x_q(c, i):
+        def xq(c, i):
             j, g = i // 2, i % 2
-            col = 256 * (j % 2)
+            cols = slice(2 * P * (j % 2), 2 * P * (j % 2 + 1))
             nc.vector.quantize_mx(
-                out=xq[c][:, j // 2, g, col:col + 256].bitcast(FP8X4),
-                scales=xs[c][:, j // 2, g, col:col + 256],
-                in_=live["stg%d%d" % (c, i)][:],
+                out=x_words[c][:, j // 2, g, cols].bitcast(FP8X4), scales=x_scales[c][:, j // 2, g, cols],
+                in_=live["xc%d%d" % (c, i)][:],
             )
 
-        def mx(c, hf, ht):
-            acc = psum.tile([P, 512], F32, tag="ps")
-            live["acc%d%d%d" % (c, hf, ht)] = acc
-            for g in range(2):
+        def mm(c, hf, ht):
+            acc = psum.tile([P, HALF], F32, tag="bank", name="acc")
+            live["mm%d%d%d" % (c, hf, ht)] = acc
+            rows = slice(P * ht, P * (ht + 1))
+            for g in range(PASSES):
                 nc.tensor.matmul_mx(
                     out=acc[:],
-                    lhsT=wq[c][:, g, P * ht:P * (ht + 1)].bitcast(FP8X4),
-                    lhsT_scale=ws[c][:, g, P * ht:P * (ht + 1)],
-                    rhs=xq[c][:, hf, g, :].bitcast(FP8X4),
-                    rhs_scale=xs[c][:, hf, g, :],
-                    start=(g == 0), stop=(g == 1),
+                    lhsT=w_words[c][:, g, rows].bitcast(FP8X4), lhsT_scale=w_scales[c][:, g, rows],
+                    rhs=x_words[c][:, hf, g, :].bitcast(FP8X4), rhs_scale=x_scales[c][:, hf, g, :],
+                    start=(g == 0), stop=(g == PASSES - 1),
                 )
 
         def ab(hf, ht):
-            t = absp.tile([P, 512], F32, tag="ab")
+            t = absp.tile([P, HALF], F32, tag="abs")
             live["ab%d%d" % (hf, ht)] = t
-            nc.scalar.activation(out=t[:], in_=live["acc0%d%d" % (hf, ht)][:], func=ACT.Abs,
+            nc.scalar.activation(out=t[:], in_=live["mm0%d%d" % (hf, ht)][:], func=ACT.Abs,
                                  bias=vec[:, ht:ht + 1], scale=1.0)
 
-        def at(hf, ht):
-            dst = a_t[:, ht, 512 * hf:512 * (hf + 1)]
-            src = live["acc0%d%d" % (hf, ht)][:]
-            if ("at%d%d" % (hf, ht)) in ON_VECTOR:
-                nc.vector.tensor_scalar(out=dst, in0=src, scalar1=keep[:, ht:ht + 1], scalar2=b1k[:, ht:ht + 1],
-                                        op0=ALU.mult, op1=ALU.add)
-            else:
-                nc.scalar.activation(out=dst, in_=src, func=ACT.Identity, bias=b1k[:, ht:ht + 1],
-                                     scale=keep[:, ht:ht + 1])
+        def am(hf, ht):
+            nc.scalar.activation(out=c_t[:, ht, HALF * hf:HALF * (hf + 1)], in_=live["mm0%d%d" % (hf, ht)][:],
+                                 func=ACT.Identity, bias=b1_kept[:, ht:ht + 1], scale=keep[:, ht:ht + 1])
 
-        def add(label):
-            hf = int(label[4])
-            hts = label[6:]
-            t = sump.tile([P, 512], F32, tag="s")
-            first = live["ab%d%s" % (hf, hts[0])] if len(hts) == 2 else live["s%d_%s" % (hf, hts[0:len(hts) - 1])]
-            live["s%d_%s" % (hf, hts)] = t
-            eng = nc.vector if ADD_ENGINE.get(label, "G") == "V" else nc.gpsimd
-            eng.tensor_tensor(out=t[:], in0=first[:], in1=live["ab%d%s" % (hf, hts[len(hts) - 1])][:], op=ALU.add)
+        sum_inputs = {"su00": ("ab00", "ab01"), "su01": ("su00", "ab02"), "su02": ("su01", "ab03"),
+                      "su10": ("ab10", "ab11"), "su11": ("ab12", "ab13")}
+        n_inputs = {"ns00": ("su02", True, True), "ns10": ("su10", True, False), "ns11": ("su11", False, True)}
 
-        def ns(hf, gi):
-            groups = NS_GROUPS[hf]
-            if gi == 0:
-                live["ns%d" % hf] = psum.tile([P, 512], F32, tag="ps", name="ns")
-            nc.tensor.matmul(out=live["ns%d" % hf][:], lhsT=plusminus[:], rhs=live["s%d_%s" % (hf, groups[gi])][:],
-                             start=(gi == 0), stop=(gi == len(groups) - 1))
+        def su(hf, k):
+            name = "su%d%d" % (hf, k)
+            t = sump.tile([P, HALF], F32, tag="sum")
+            live[name] = t
+            nc.vector.tensor_tensor(out=t[:], in0=live[sum_inputs[name][0]][:], in1=live[sum_inputs[name][1]][:],
+                                    op=ALU.add)
 
-        def red(hf):
-            nc.vector.tensor_reduce(out=r2[:, hf:hf + 1], in_=live["ns%d" % hf][:], axis=AX.X, op=ALU.max)
+        def ns(hf, k):
+            source, start, stop = n_inputs["ns%d%d" % (hf, k)]
+            if start:
+                live["ns%d" % hf] = psum.tile([P, HALF], F32, tag="bank", name="n_signed")
+            nc.tensor.matmul(out=live["ns%d" % hf][:], lhsT=plus_minus[:], rhs=live[source][:], start=start, stop=stop)
 
-        def rmax():
-            nc.vector.tensor_tensor(out=rr2[:], in0=r2[:, 0:1].to_broadcast([P, 2]),
-                                    in1=r2[:, 1:2].to_broadcast([P, 2]), op=ALU.max)
+        def rd(hf):
+            nc.vector.tensor_reduce(out=half_max[:, hf:hf + 1], in_=live["ns%d" % hf][:], axis=AX.X, op=ALU.max)
 
-        def sens():
-            live["sens"] = psum.tile([P, 2], F32, tag="ps", name="sens")
-            nc.tensor.matmul(out=live["sens"][:], lhsT=pick[:], rhs=rr2[:], start=True, stop=True)
+        def rm():
+            nc.vector.tensor_tensor(out=both_max[:], in0=half_max[:, 0:1].to_broadcast([P, 2]),
+                                    in1=half_max[:, 1:2].to_broadcast([P, 2]), op=ALU.max)
 
-        def mk_v():
-            nc.vector.tensor_tensor(out=mk[:], in0=live["sens"][:, 0:1].to_broadcast([P, 4]), in1=keep_e[:],
-                                    op=ALU.mult)
+        def se():
+            live["se"] = psum.tile([P, 2], F32, tag="bank", name="sens")
+            nc.tensor.matmul(out=live["se"][:], lhsT=pick[:], rhs=both_max[:], start=True, stop=True)
 
-        def n_t(hf, hp):
-            nz = psum.tile([P, 2, 512], BF16, tag="ps")
-            live["nz%d%d" % (hf, hp)] = nz
+        def mk():
+            nc.vector.tensor_tensor(out=noise_scale[:], in0=live["se"][:, 0:1].to_broadcast([P, H_TILES]),
+                                    in1=keep_over_eps[:], op=ALU.mult)
+
+        def nt(hf, hp):
+            bank = psum.tile([P, 2, HALF], BF16, tag="bank", name="noise_t")
+            live["nt%d%d" % (hf, hp)] = bank
             for a in range(2):
                 ht = 2 * hp + a
                 for tt in range(4):
-                    nc.tensor.transpose(nz[:, a, P * tt:P * (tt + 1)],
-                                        nraw[:, 4 * hf + tt, P * ht:P * (ht + 1)], ident_b[:])
+                    nc.tensor.transpose(bank[:, a, P * tt:P * (tt + 1)],
+                                        noise[:, 4 * hf + tt, P * ht:P * (ht + 1)], ident_b[:])
 
-        def c_t(hf, ht):
-            sl = a_t[:, ht, 512 * hf:512 * (hf + 1)]
-            nc.vector.scalar_tensor_tensor(out=sl, in0=live["nz%d%d" % (hf, ht // 2)][:, ht % 2, :],
-                                           scalar=mk[:, ht:ht + 1], in1=sl, op0=ALU.mult, op1=ALU.add)
+        def ct(hf, ht):
+            part = c_t[:, ht, HALF * hf:HALF * (hf + 1)]
+            nc.vector.scalar_tensor_tensor(out=part, in0=live["nt%d%d" % (hf, ht // 2)][:, ht % 2, :],
+                                           scalar=noise_scale[:, ht:ht + 1], in1=part, op0=ALU.mult, op1=ALU.add)
 
-        def o_t(hf, ht):
-            t = outp.tile([P, 512], F32, tag="o_t")
-            live["oT%d%d" % (hf, ht)] = t
-            nc.vector.scalar_tensor_tensor(out=t[:], in0=live["acc1%d%d" % (hf, ht)][:],
+        def mn(hf, ht):
+            t = outp.tile([P, HALF], F32, tag="min")
+            live["mn%d%d" % (hf, ht)] = t
+            nc.vector.scalar_tensor_tensor(out=t[:], in0=live["mm1%d%d" % (hf, ht)][:],
                                            scalar=vec[:, 4 + ht:5 + ht],
-                                           in1=a_t[:, ht, 512 * hf:512 * (hf + 1)], op0=ALU.add, op1=ALU.min)
+                                           in1=c_t[:, ht, HALF * hf:HALF * (hf + 1)], op0=ALU.add, op1=ALU.min)
 
-        def o_tr(hf, ht):
-            ot = psum.tile([P, 4, P], F32, tag="ps")
-            live["ot%d%d" % (hf, ht)] = ot
+        def tr(hf, ht):
+            bank = psum.tile([P, 4, P], F32, tag="bank", name="out_t")
+            live["tr%d%d" % (hf, ht)] = bank
             for tt in range(4):
-                nc.tensor.transpose(ot[:, tt, :], live["oT%d%d" % (hf, ht)][:, P * tt:P * (tt + 1)], ident_f[:])
+                nc.tensor.transpose(bank[:, tt, :], live["mn%d%d" % (hf, ht)][:, P * tt:P * (tt + 1)], ident_f[:])
 
-        def o_c(hf, ht):
-            cols = slice(P * ht, P * (ht + 1))
+        def oc(hf, ht):
             rows = slice(4 * hf, 4 * hf + 4)
-            copy_engine("oC%d%d" % (hf, ht))(out=osb[:, rows, cols], in_=live["ot%d%d" % (hf, ht)][:])
-            nc.sync.dma_start(out=outv[:, rows, cols], in_=osb[:, rows, cols])
+            cols = slice(P * ht, P * (ht + 1))
+            psum_copy("oc%d%d" % (hf, ht))(out=out_rows[:, rows, cols], in_=live["tr%d%d" % (hf, ht)][:])
 
-        two = {"wR": w_regroup, "wQ": w_quant, "xT": x_t, "xC": x_c, "xQ": x_q, "ab": ab, "at": at, "ns": ns,
-               "nT": n_t, "cT": c_t, "oT": o_t, "oR": o_tr, "oC": o_c}
-        for label in ORDER:
-            if label == "vecT":
-                vec_t()
-            elif label == "vec":
-                vec_v()
-            elif label == "rmax":
-                rmax()
-            elif label == "sens":
-                sens()
-            elif label == "mk":
-                mk_v()
-            elif label[0:3] == "red":
-                red(int(label[3]))
-            elif label[0:3] == "add":
-                add(label)
-            elif label[0] == "m":
-                mx(int(label[1]), int(label[2]), int(label[3]))
-            else:
-                two[label[0:2]](int(label[2]), int(label[3]))
+        def st(hf, ht):
+            rows = slice(4 * hf, 4 * hf + 4)
+            cols = slice(P * ht, P * (ht + 1))
+            nc.sync.dma_start(out=out_view[:, rows, cols], in_=out_rows[:, rows, cols])
+
+        steps = {"vt": (vt, (), []), "vv": (vv, (), ["vt"]), "rm": (rm, (), ["rd0", "rd1"]), "se": (se, (), ["rm"]),
+                 "mk": (mk, (), ["se", "vv"])}
+        for c in range(2):
+            for g in range(PASSES):
+                steps["wr%d%d" % (c, g)] = (wr, (c, g), [])
+                steps["wq%d%d" % (c, g)] = (wq, (c, g), ["wr%d%d" % (c, g)])
+            for i in range(8):
+                steps["xt%d%d" % (c, i)] = (xt, (c, i), [])
+                steps["xc%d%d" % (c, i)] = (xc, (c, i), ["xt%d%d" % (c, i)])
+                steps["xq%d%d" % (c, i)] = (xq, (c, i), ["xc%d%d" % (c, i)])
+            for hf in range(2):
+                operands = names("wq%d" % c, 0, 1) + names("xq%d" % c, 4 * hf, 4 * hf + 3)
+                for ht in range(H_TILES):
+                    steps["mm%d%d%d" % (c, hf, ht)] = (mm, (c, hf, ht), operands)
+        for name in sum_inputs:
+            steps[name] = (su, (int(name[2]), int(name[3])), list(sum_inputs[name]))
+        for name in n_inputs:
+            steps[name] = (ns, (int(name[2]), int(name[3])), [n_inputs[name][0]])
+        steps["ns11"][2].append("ns10")
+        steps["rd0"] = (rd, (0,), ["ns00"])
+        steps["rd1"] = (rd, (1,), ["ns11"])
+        for hf in range(2):
+            for hp in range(2):
+                steps["nt%d%d" % (hf, hp)] = (nt, (hf, hp), [])
+            for ht in range(H_TILES):
+                tile_id = "%d%d" % (hf, ht)
+                steps["ab" + tile_id] = (ab, (hf, ht), ["mm0" + tile_id, "vv"])
+                steps["am" + tile_id] = (am, (hf, ht), ["mm0" + tile_id, "vv"])
+                steps["ct" + tile_id] = (ct, (hf, ht), ["nt%d%d" % (hf, ht // 2), "mk", "am" + tile_id])
+                steps["mn" + tile_id] = (mn, (hf, ht), ["mm1" + tile_id, "ct" + tile_id])
+                steps["tr" + tile_id] = (tr, (hf, ht), ["mn" + tile_id])
+                steps["oc" + tile_id] = (oc, (hf, ht), ["tr" + tile_id])
+                steps["st" + tile_id] = (st, (hf, ht), ["oc" + tile_id])
+
+        queues = [tensor_queue, vector_queue, scalar_queue, sync_queue]
+        assert sorted(tensor_queue + vector_queue + scalar_queue + sync_queue) == sorted(steps)
+        heads = [0, 0, 0, 0]
+        written = set()
+        while len(written) < len(steps):
+            before = len(written)
+            for k in range(4):
+                while heads[k] < len(queues[k]) and all(need in written for need in steps[queues[k][heads[k]]][2]):
+                    function, arguments, needs = steps[queues[k][heads[k]]]
+                    function(*arguments)
+                    written.add(queues[k][heads[k]])
+                    heads[k] += 1
+            assert len(written) > before, "the queues wait for each other"

@@ -15,9 +15,9 @@ AX = mybir.AxisListType
 P = 128
 B, F, H = 1024, 1024, 512
 FLOPS = 2 * 2 * B * F * H
-TILES = B // P
+BATCH_TILES = B // P
 PASSES = F // (4 * P)
-H_TILES = H // P
+FEATURE_TILES = H // P
 HALF = 512
 INV_EPS = 7.5
 P_KEEP = 0.95
@@ -57,18 +57,18 @@ def tile_splitnn_pa_kernel(tc, x1, x2, W1, b1, W2, b2, noise_std, rr_uniform, ou
     with ExitStack() as ctx:
         ctx.enter_context(tc.manual_schedule())
         const = ctx.enter_context(tc.tile_pool(name="const", bufs=1))
-        stage = ctx.enter_context(tc.tile_pool(name="stage", bufs=6))
-        absp = ctx.enter_context(tc.tile_pool(name="absp", bufs=8))
-        sump = ctx.enter_context(tc.tile_pool(name="sump", bufs=4))
-        outp = ctx.enter_context(tc.tile_pool(name="outp", bufs=8))
+        group_pool = ctx.enter_context(tc.tile_pool(name="group_pool", bufs=6))
+        abs_pool = ctx.enter_context(tc.tile_pool(name="abs_pool", bufs=8))
+        sum_pool = ctx.enter_context(tc.tile_pool(name="sum_pool", bufs=4))
+        min_pool = ctx.enter_context(tc.tile_pool(name="min_pool", bufs=8))
         psum = ctx.enter_context(tc.psum_pool(name="psum", bufs=8))
 
-        ident_f = const.tile([P, P], F32)
-        make_identity(nc, ident_f[:])
-        ident_b = const.tile([P, P], BF16)
-        make_identity(nc, ident_b[:])
-        vec_rows = const.tile([P, P], BF16)
-        nc.vector.memset(vec_rows[:], 0.0)
+        ident_f32 = const.tile([P, P], F32)
+        make_identity(nc, ident_f32[:])
+        ident_bf16 = const.tile([P, P], BF16)
+        make_identity(nc, ident_bf16[:])
+        vector_rows = const.tile([P, P], BF16)
+        nc.vector.memset(vector_rows[:], 0.0)
         plus_minus = const.tile([P, P], F32)
         nc.vector.memset(plus_minus[:, 0:64], 1.0)
         nc.vector.memset(plus_minus[:, 64:128], -1.0)
@@ -76,150 +76,150 @@ def tile_splitnn_pa_kernel(tc, x1, x2, W1, b1, W2, b2, noise_std, rr_uniform, ou
         nc.vector.memset(pick[:], 0.0)
         nc.vector.memset(pick[0:1, :], 1.0)
         nc.vector.memset(pick[64:65, :], 1.0)
-        zero_col = const.tile([P, 1], F32)
-        nc.vector.memset(zero_col[:], 0.0)
-        table_warm = const.tile([P, 1], F32)
-        nc.scalar.activation(out=table_warm[:], in_=zero_col[:], func=ACT.Abs)
+        zero_column = const.tile([P, 1], F32)
+        nc.vector.memset(zero_column[:], 0.0)
+        early_abs = const.tile([P, 1], F32)
+        nc.scalar.activation(out=early_abs[:], in_=zero_column[:], func=ACT.Abs)
 
-        nc.sync.dma_start(out=vec_rows[0:4, :], in_=b1.rearrange("(r c) -> r c", c=P))
-        nc.sync.dma_start(out=vec_rows[4:8, :], in_=b2.rearrange("(r c) -> r c", c=P))
-        nc.sync.dma_start(out=vec_rows[8:12, :], in_=rr_uniform.rearrange("(r c) -> r c", c=P))
+        nc.sync.dma_start(out=vector_rows[0:4, :], in_=b1.rearrange("(r v) -> r v", v=P))
+        nc.sync.dma_start(out=vector_rows[4:8, :], in_=b2.rearrange("(r v) -> r v", v=P))
+        nc.sync.dma_start(out=vector_rows[8:12, :], in_=rr_uniform.rearrange("(r v) -> r v", v=P))
 
         w_raw = [const.tile([P, PASSES, 4, H], BF16, name="w_raw%d" % c) for c in range(2)]
-        x_raw = [const.tile([P, TILES * F], BF16, name="x_raw%d" % c) for c in range(2)]
-        noise = const.tile([P, TILES, H], BF16)
+        x_raw = [const.tile([P, BATCH_TILES * F], BF16, name="x_raw%d" % c) for c in range(2)]
+        noise = const.tile([P, BATCH_TILES, H], BF16)
 
         def load_w(c, w, g):
             nc.sync.dma_start(
-                out=w_raw[c][:, g].rearrange("q (u e) h -> q u (e h)", u=2),
-                in_=w[512 * g:512 * (g + 1), :].rearrange("(u q e) h -> q u (e h)", u=2, e=2),
+                out=w_raw[c][:, g].rearrange("q (u e) j -> q u (e j)", u=2),
+                in_=w[512 * g:512 * (g + 1), :].rearrange("(u q e) j -> q u (e j)", u=2, e=2),
             )
 
-        def load_x(c, x, j):
-            cols = slice(2 * F * j, 2 * F * (j + 1))
-            nc.sync.dma_start(out=x_raw[c][:, cols], in_=x.rearrange("(p t) k -> p (t k)", t=TILES)[:, cols])
+        def load_x(c, x, pair):
+            span = slice(2 * F * pair, 2 * F * (pair + 1))
+            nc.sync.dma_start(out=x_raw[c][:, span], in_=x.rearrange("(p t) k -> p (t k)", t=BATCH_TILES)[:, span])
 
         load_w(0, W1, 0)
         load_x(0, x1, 0)
         load_w(0, W1, 1)
-        for j in range(1, 4):
-            load_x(0, x1, j)
+        for pair in range(1, 4):
+            load_x(0, x1, pair)
         load_w(1, W2, 0)
         load_w(1, W2, 1)
-        for j in range(4):
-            load_x(1, x2, j)
-        nc.sync.dma_start(out=noise[:], in_=noise_std.rearrange("(p t) h -> p t h", t=TILES))
+        for pair in range(4):
+            load_x(1, x2, pair)
+        nc.sync.dma_start(out=noise[:], in_=noise_std.rearrange("(p t) j -> p t j", t=BATCH_TILES))
 
         w_grouped = [const.tile([P, PASSES, H, 4], BF16, name="w_grouped%d" % c, align_bytes=64) for c in range(2)]
         w_words = [const.tile([P, PASSES, H], U32, name="w_words%d" % c, align_bytes=64) for c in range(2)]
         w_scales = [const.tile([P, PASSES, H], U8, name="w_scales%d" % c, align_bytes=64) for c in range(2)]
         x_words = [const.tile([P, 2, PASSES, HALF], U32, name="x_words%d" % c, align_bytes=64) for c in range(2)]
         x_scales = [const.tile([P, 2, PASSES, HALF], U8, name="x_scales%d" % c, align_bytes=64) for c in range(2)]
-        vec = const.tile([P, 12], F32)
-        keep = const.tile([P, H_TILES], F32)
-        b1_kept = const.tile([P, H_TILES], F32)
-        keep_over_eps = const.tile([P, H_TILES], F32)
-        noise_scale = const.tile([P, H_TILES], F32)
-        c_t = const.tile([P, H_TILES, B], F32)
+        vectors = const.tile([P, 3 * FEATURE_TILES], F32)
+        keep = const.tile([P, FEATURE_TILES], F32)
+        b1_kept = const.tile([P, FEATURE_TILES], F32)
+        keep_over_eps = const.tile([P, FEATURE_TILES], F32)
+        noise_scale = const.tile([P, FEATURE_TILES], F32)
+        c_t = const.tile([P, FEATURE_TILES, B], F32)
         half_max = const.tile([P, 2], F32)
         both_max = const.tile([P, 2], F32)
-        out_rows = const.tile([P, TILES, H], F32)
-        out_view = out.rearrange("(p t) h -> p t h", t=TILES)
+        out_rows = const.tile([P, BATCH_TILES, H], F32)
+        out_view = out.rearrange("(p t) j -> p t j", t=BATCH_TILES)
         live = {}
 
-        def psum_copy(name):
-            return nc.vector.tensor_copy if name in vector_queue else nc.scalar.copy
+        def copy_on_its_engine(step_name):
+            return nc.vector.tensor_copy if step_name in vector_queue else nc.scalar.copy
 
         def vt():
-            live["vt"] = psum.tile([P, P], BF16, tag="bank", name="vec_t")
-            nc.tensor.transpose(live["vt"][:], vec_rows[:], ident_b[:])
+            live["vt"] = psum.tile([P, P], BF16, tag="bank", name="vectors_t")
+            nc.tensor.transpose(live["vt"][:], vector_rows[:], ident_bf16[:])
 
         def vv():
-            nc.vector.tensor_copy(out=vec[:], in_=live["vt"][:, 0:12])
-            nc.vector.tensor_single_scalar(out=keep[:], in_=vec[:, 8:12], scalar=P_KEEP, op=ALU.is_lt)
-            nc.vector.tensor_tensor(out=b1_kept[:], in0=vec[:, 0:4], in1=keep[:], op=ALU.mult)
+            nc.vector.tensor_copy(out=vectors[:], in_=live["vt"][:, 0:3 * FEATURE_TILES])
+            nc.vector.tensor_single_scalar(out=keep[:], in_=vectors[:, 8:12], scalar=P_KEEP, op=ALU.is_lt)
+            nc.vector.tensor_tensor(out=b1_kept[:], in0=vectors[:, 0:4], in1=keep[:], op=ALU.mult)
             nc.vector.tensor_single_scalar(out=keep_over_eps[:], in_=keep[:], scalar=INV_EPS, op=ALU.mult)
 
         def wr(c, g):
             nc.vector.tensor_copy(
-                out=w_grouped[c][:, g].rearrange("p (c i) t -> p c t i", i=4),
-                in_=w_raw[c][:, g].rearrange("p t (c i) -> p c t i", i=4),
+                out=w_grouped[c][:, g].rearrange("q (n i) v -> q n v i", i=4),
+                in_=w_raw[c][:, g].rearrange("q v (n i) -> q n v i", i=4),
             )
 
         def wq(c, g):
             nc.vector.quantize_mx(
                 out=w_words[c][:, g, :].bitcast(FP8X4), scales=w_scales[c][:, g, :],
-                in_=w_grouped[c][:, g].rearrange("p h t -> p (h t)"),
+                in_=w_grouped[c][:, g].rearrange("q j v -> q (j v)"),
             )
 
         def xt(c, i):
-            j, g = i // 2, i % 2
+            pair, g = i // 2, i % 2
             words = x_raw[c][:].bitcast(F32)
             bank = psum.tile([P, 2, 2, P], F32, tag="bank", name="x_t")
             live["xt%d%d" % (c, i)] = bank
-            for tt in range(2):
+            for s in range(2):
                 for u in range(2):
-                    first = (F // 2) * (2 * j + tt) + 256 * g + P * u
-                    nc.tensor.transpose(bank[:, tt, u, :], words[:, first:first + P], ident_f[:])
+                    first = (F // 2) * (2 * pair + s) + 256 * g + P * u
+                    nc.tensor.transpose(bank[:, s, u, :], words[:, first:first + P], ident_f32[:])
 
         def xc(c, i):
-            name = "xc%d%d" % (c, i)
-            grouped = stage.tile([P, 4 * 2 * P], BF16, tag="grouped", align_bytes=64)
-            live[name] = grouped
-            psum_copy(name)(
-                out=grouped[:].bitcast(F32).rearrange("q (tt r u) -> q tt r u", tt=2, u=2),
-                in_=live["xt%d%d" % (c, i)][:].rearrange("q tt u r -> q tt r u"),
+            step_name = "xc%d%d" % (c, i)
+            grouped = group_pool.tile([P, 4 * 2 * P], BF16, tag="grouped", align_bytes=64)
+            live[step_name] = grouped
+            copy_on_its_engine(step_name)(
+                out=grouped[:].bitcast(F32).rearrange("q (s r u) -> q s r u", s=2, u=2),
+                in_=live["xt%d%d" % (c, i)][:].rearrange("q s u r -> q s r u"),
             )
 
         def xq(c, i):
-            j, g = i // 2, i % 2
-            cols = slice(2 * P * (j % 2), 2 * P * (j % 2 + 1))
+            pair, g = i // 2, i % 2
+            span = slice(2 * P * (pair % 2), 2 * P * (pair % 2 + 1))
             nc.vector.quantize_mx(
-                out=x_words[c][:, j // 2, g, cols].bitcast(FP8X4), scales=x_scales[c][:, j // 2, g, cols],
+                out=x_words[c][:, pair // 2, g, span].bitcast(FP8X4), scales=x_scales[c][:, pair // 2, g, span],
                 in_=live["xc%d%d" % (c, i)][:],
             )
 
-        def mm(c, hf, ht):
+        def mm(c, f, h):
             acc = psum.tile([P, HALF], F32, tag="bank", name="acc")
-            live["mm%d%d%d" % (c, hf, ht)] = acc
-            rows = slice(P * ht, P * (ht + 1))
+            live["mm%d%d%d" % (c, f, h)] = acc
+            features = slice(P * h, P * (h + 1))
             for g in range(PASSES):
                 nc.tensor.matmul_mx(
                     out=acc[:],
-                    lhsT=w_words[c][:, g, rows].bitcast(FP8X4), lhsT_scale=w_scales[c][:, g, rows],
-                    rhs=x_words[c][:, hf, g, :].bitcast(FP8X4), rhs_scale=x_scales[c][:, hf, g, :],
+                    lhsT=w_words[c][:, g, features].bitcast(FP8X4), lhsT_scale=w_scales[c][:, g, features],
+                    rhs=x_words[c][:, f, g, :].bitcast(FP8X4), rhs_scale=x_scales[c][:, f, g, :],
                     start=(g == 0), stop=(g == PASSES - 1),
                 )
 
-        def ab(hf, ht):
-            t = absp.tile([P, HALF], F32, tag="abs")
-            live["ab%d%d" % (hf, ht)] = t
-            nc.scalar.activation(out=t[:], in_=live["mm0%d%d" % (hf, ht)][:], func=ACT.Abs,
-                                 bias=vec[:, ht:ht + 1], scale=1.0)
+        def ab(f, h):
+            abs_a = abs_pool.tile([P, HALF], F32, tag="abs_a")
+            live["ab%d%d" % (f, h)] = abs_a
+            nc.scalar.activation(out=abs_a[:], in_=live["mm0%d%d" % (f, h)][:], func=ACT.Abs,
+                                 bias=vectors[:, h:h + 1], scale=1.0)
 
-        def am(hf, ht):
-            nc.scalar.activation(out=c_t[:, ht, HALF * hf:HALF * (hf + 1)], in_=live["mm0%d%d" % (hf, ht)][:],
-                                 func=ACT.Identity, bias=b1_kept[:, ht:ht + 1], scale=keep[:, ht:ht + 1])
+        def am(f, h):
+            nc.scalar.activation(out=c_t[:, h, HALF * f:HALF * (f + 1)], in_=live["mm0%d%d" % (f, h)][:],
+                                 func=ACT.Identity, bias=b1_kept[:, h:h + 1], scale=keep[:, h:h + 1])
 
         sum_inputs = {"su00": ("ab00", "ab01"), "su01": ("su00", "ab02"), "su02": ("su01", "ab03"),
                       "su10": ("ab10", "ab11"), "su11": ("ab12", "ab13")}
         n_inputs = {"ns00": ("su02", True, True), "ns10": ("su10", True, False), "ns11": ("su11", False, True)}
 
-        def su(hf, k):
-            name = "su%d%d" % (hf, k)
-            t = sump.tile([P, HALF], F32, tag="sum")
-            live[name] = t
-            nc.vector.tensor_tensor(out=t[:], in0=live[sum_inputs[name][0]][:], in1=live[sum_inputs[name][1]][:],
-                                    op=ALU.add)
+        def su(f, n):
+            step_name = "su%d%d" % (f, n)
+            partial = sum_pool.tile([P, HALF], F32, tag="partial")
+            live[step_name] = partial
+            nc.vector.tensor_tensor(out=partial[:], in0=live[sum_inputs[step_name][0]][:],
+                                    in1=live[sum_inputs[step_name][1]][:], op=ALU.add)
 
-        def ns(hf, k):
-            source, start, stop = n_inputs["ns%d%d" % (hf, k)]
+        def ns(f, n):
+            source, start, stop = n_inputs["ns%d%d" % (f, n)]
             if start:
-                live["ns%d" % hf] = psum.tile([P, HALF], F32, tag="bank", name="n_signed")
-            nc.tensor.matmul(out=live["ns%d" % hf][:], lhsT=plus_minus[:], rhs=live[source][:], start=start, stop=stop)
+                live["ns%d" % f] = psum.tile([P, HALF], F32, tag="bank", name="n_signed")
+            nc.tensor.matmul(out=live["ns%d" % f][:], lhsT=plus_minus[:], rhs=live[source][:], start=start, stop=stop)
 
-        def rd(hf):
-            nc.vector.tensor_reduce(out=half_max[:, hf:hf + 1], in_=live["ns%d" % hf][:], axis=AX.X, op=ALU.max)
+        def rd(f):
+            nc.vector.tensor_reduce(out=half_max[:, f:f + 1], in_=live["ns%d" % f][:], axis=AX.X, op=ALU.max)
 
         def rm():
             nc.vector.tensor_tensor(out=both_max[:], in0=half_max[:, 0:1].to_broadcast([P, 2]),
@@ -230,48 +230,47 @@ def tile_splitnn_pa_kernel(tc, x1, x2, W1, b1, W2, b2, noise_std, rr_uniform, ou
             nc.tensor.matmul(out=live["se"][:], lhsT=pick[:], rhs=both_max[:], start=True, stop=True)
 
         def mk():
-            nc.vector.tensor_tensor(out=noise_scale[:], in0=live["se"][:, 0:1].to_broadcast([P, H_TILES]),
+            nc.vector.tensor_tensor(out=noise_scale[:], in0=live["se"][:, 0:1].to_broadcast([P, FEATURE_TILES]),
                                     in1=keep_over_eps[:], op=ALU.mult)
 
-        def nt(hf, hp):
+        def nt(f, p):
             bank = psum.tile([P, 2, HALF], BF16, tag="bank", name="noise_t")
-            live["nt%d%d" % (hf, hp)] = bank
-            for a in range(2):
-                ht = 2 * hp + a
-                for tt in range(4):
-                    nc.tensor.transpose(bank[:, a, P * tt:P * (tt + 1)],
-                                        noise[:, 4 * hf + tt, P * ht:P * (ht + 1)], ident_b[:])
+            live["nt%d%d" % (f, p)] = bank
+            for s in range(2):
+                h = 2 * p + s
+                for t in range(4):
+                    nc.tensor.transpose(bank[:, s, P * t:P * (t + 1)],
+                                        noise[:, 4 * f + t, P * h:P * (h + 1)], ident_bf16[:])
 
-        def ct(hf, ht):
-            part = c_t[:, ht, HALF * hf:HALF * (hf + 1)]
-            nc.vector.scalar_tensor_tensor(out=part, in0=live["nt%d%d" % (hf, ht // 2)][:, ht % 2, :],
-                                           scalar=noise_scale[:, ht:ht + 1], in1=part, op0=ALU.mult, op1=ALU.add)
+        def ct(f, h):
+            part = c_t[:, h, HALF * f:HALF * (f + 1)]
+            nc.vector.scalar_tensor_tensor(out=part, in0=live["nt%d%d" % (f, h // 2)][:, h % 2, :],
+                                           scalar=noise_scale[:, h:h + 1], in1=part, op0=ALU.mult, op1=ALU.add)
 
-        def mn(hf, ht):
-            t = outp.tile([P, HALF], F32, tag="min")
-            live["mn%d%d" % (hf, ht)] = t
-            nc.vector.scalar_tensor_tensor(out=t[:], in0=live["mm1%d%d" % (hf, ht)][:],
-                                           scalar=vec[:, 4 + ht:5 + ht],
-                                           in1=c_t[:, ht, HALF * hf:HALF * (hf + 1)], op0=ALU.add, op1=ALU.min)
+        def mn(f, h):
+            smaller = min_pool.tile([P, HALF], F32, tag="smaller")
+            live["mn%d%d" % (f, h)] = smaller
+            nc.vector.scalar_tensor_tensor(out=smaller[:], in0=live["mm1%d%d" % (f, h)][:],
+                                           scalar=vectors[:, 4 + h:5 + h],
+                                           in1=c_t[:, h, HALF * f:HALF * (f + 1)], op0=ALU.add, op1=ALU.min)
 
-        def tr(hf, ht):
+        def tr(f, h):
             bank = psum.tile([P, 4, P], F32, tag="bank", name="out_t")
-            live["tr%d%d" % (hf, ht)] = bank
-            for tt in range(4):
-                nc.tensor.transpose(bank[:, tt, :], live["mn%d%d" % (hf, ht)][:, P * tt:P * (tt + 1)], ident_f[:])
+            live["tr%d%d" % (f, h)] = bank
+            for t in range(4):
+                nc.tensor.transpose(bank[:, t, :], live["mn%d%d" % (f, h)][:, P * t:P * (t + 1)], ident_f32[:])
 
-        def oc(hf, ht):
-            rows = slice(4 * hf, 4 * hf + 4)
-            cols = slice(P * ht, P * (ht + 1))
-            psum_copy("oc%d%d" % (hf, ht))(out=out_rows[:, rows, cols], in_=live["tr%d%d" % (hf, ht)][:])
+        def oc(f, h):
+            copy_on_its_engine("oc%d%d" % (f, h))(
+                out=out_rows[:, 4 * f:4 * f + 4, P * h:P * (h + 1)], in_=live["tr%d%d" % (f, h)][:]
+            )
 
-        def st(hf, ht):
-            rows = slice(4 * hf, 4 * hf + 4)
-            cols = slice(P * ht, P * (ht + 1))
-            nc.sync.dma_start(out=out_view[:, rows, cols], in_=out_rows[:, rows, cols])
+        def st(f, h):
+            nc.sync.dma_start(out=out_view[:, 4 * f:4 * f + 4, P * h:P * (h + 1)],
+                              in_=out_rows[:, 4 * f:4 * f + 4, P * h:P * (h + 1)])
 
         steps = {"vt": (vt, (), []), "vv": (vv, (), ["vt"]), "rm": (rm, (), ["rd0", "rd1"]), "se": (se, (), ["rm"]),
-                 "mk": (mk, (), ["se", "vv"])}
+                 "mk": (mk, (), ["se", "vv"]), "rd0": (rd, (0,), ["ns00"]), "rd1": (rd, (1,), ["ns11"])}
         for c in range(2):
             for g in range(PASSES):
                 steps["wr%d%d" % (c, g)] = (wr, (c, g), [])
@@ -280,29 +279,27 @@ def tile_splitnn_pa_kernel(tc, x1, x2, W1, b1, W2, b2, noise_std, rr_uniform, ou
                 steps["xt%d%d" % (c, i)] = (xt, (c, i), [])
                 steps["xc%d%d" % (c, i)] = (xc, (c, i), ["xt%d%d" % (c, i)])
                 steps["xq%d%d" % (c, i)] = (xq, (c, i), ["xc%d%d" % (c, i)])
-            for hf in range(2):
-                operands = names("wq%d" % c, 0, 1) + names("xq%d" % c, 4 * hf, 4 * hf + 3)
-                for ht in range(H_TILES):
-                    steps["mm%d%d%d" % (c, hf, ht)] = (mm, (c, hf, ht), operands)
-        for name in sum_inputs:
-            steps[name] = (su, (int(name[2]), int(name[3])), list(sum_inputs[name]))
-        for name in n_inputs:
-            steps[name] = (ns, (int(name[2]), int(name[3])), [n_inputs[name][0]])
+            for f in range(2):
+                operands = names("wq%d" % c, 0, 1) + names("xq%d" % c, 4 * f, 4 * f + 3)
+                for h in range(FEATURE_TILES):
+                    steps["mm%d%d%d" % (c, f, h)] = (mm, (c, f, h), operands)
+        for step_name in sum_inputs:
+            steps[step_name] = (su, (int(step_name[2]), int(step_name[3])), list(sum_inputs[step_name]))
+        for step_name in n_inputs:
+            steps[step_name] = (ns, (int(step_name[2]), int(step_name[3])), [n_inputs[step_name][0]])
         steps["ns11"][2].append("ns10")
-        steps["rd0"] = (rd, (0,), ["ns00"])
-        steps["rd1"] = (rd, (1,), ["ns11"])
-        for hf in range(2):
-            for hp in range(2):
-                steps["nt%d%d" % (hf, hp)] = (nt, (hf, hp), [])
-            for ht in range(H_TILES):
-                tile_id = "%d%d" % (hf, ht)
-                steps["ab" + tile_id] = (ab, (hf, ht), ["mm0" + tile_id, "vv"])
-                steps["am" + tile_id] = (am, (hf, ht), ["mm0" + tile_id, "vv"])
-                steps["ct" + tile_id] = (ct, (hf, ht), ["nt%d%d" % (hf, ht // 2), "mk", "am" + tile_id])
-                steps["mn" + tile_id] = (mn, (hf, ht), ["mm1" + tile_id, "ct" + tile_id])
-                steps["tr" + tile_id] = (tr, (hf, ht), ["mn" + tile_id])
-                steps["oc" + tile_id] = (oc, (hf, ht), ["tr" + tile_id])
-                steps["st" + tile_id] = (st, (hf, ht), ["oc" + tile_id])
+        for f in range(2):
+            for p in range(2):
+                steps["nt%d%d" % (f, p)] = (nt, (f, p), [])
+            for h in range(FEATURE_TILES):
+                fh = "%d%d" % (f, h)
+                steps["ab" + fh] = (ab, (f, h), ["mm0" + fh, "vv"])
+                steps["am" + fh] = (am, (f, h), ["mm0" + fh, "vv"])
+                steps["ct" + fh] = (ct, (f, h), ["nt%d%d" % (f, h // 2), "mk", "am" + fh])
+                steps["mn" + fh] = (mn, (f, h), ["mm1" + fh, "ct" + fh])
+                steps["tr" + fh] = (tr, (f, h), ["mn" + fh])
+                steps["oc" + fh] = (oc, (f, h), ["tr" + fh])
+                steps["st" + fh] = (st, (f, h), ["oc" + fh])
 
         queues = [tensor_queue, vector_queue, scalar_queue, sync_queue]
         assert sorted(tensor_queue + vector_queue + scalar_queue + sync_queue) == sorted(steps)
@@ -310,10 +307,11 @@ def tile_splitnn_pa_kernel(tc, x1, x2, W1, b1, W2, b2, noise_std, rr_uniform, ou
         written = set()
         while len(written) < len(steps):
             before = len(written)
-            for k in range(4):
-                while heads[k] < len(queues[k]) and all(need in written for need in steps[queues[k][heads[k]]][2]):
-                    function, arguments, needs = steps[queues[k][heads[k]]]
+            for turn in range(4):
+                queue = queues[turn]
+                while heads[turn] < len(queue) and all(need in written for need in steps[queue[heads[turn]]][2]):
+                    function, arguments, needs = steps[queue[heads[turn]]]
                     function(*arguments)
-                    written.add(queues[k][heads[k]])
-                    heads[k] += 1
+                    written.add(queue[heads[turn]])
+                    heads[turn] += 1
             assert len(written) > before, "the queues wait for each other"

@@ -29,23 +29,21 @@ def names(prefix, first, last):
 
 def engine_queues():
     tensor = (
-        ["xt00", "xt01", "vt"] + names("xt0", 2, 6) + names("mm00", 0, 2) + ["xt07", "mm003", "xt10"]
-        + names("mm01", 0, 3) + names("xt1", 1, 3) + ["ns00", "ns10", "ns11"] + names("xt1", 4, 6)
-        + ["se", "nt00", "nt01", "nt10", "xt17"] + names("mm10", 0, 2)
-        + ["nt11", "tr00", "mm103", "tr01", "mm110", "tr02", "tr03", "mm111", "mm112", "tr10", "mm113"]
-        + names("tr1", 1, 3)
+        ["xt00", "xt01", "vt"] + names("xt0", 2, 7) + names("mm00", 0, 3) + names("mm01", 0, 3) + names("mm02", 0, 3)
+        + ["ta00", "ta01"] + names("mm03", 0, 3) + ["ta02", "ta03", "xt10", "xt11"] + names("ta1", 0, 3)
+        + names("xt1", 2, 5) + ["bc", "nt00", "nt01"] + names("mm10", 0, 3) + names("mm11", 0, 3)
+        + ["xt16", "xt17", "nt10", "nt11", "tr00", "tr01"] + names("mm12", 0, 3) + ["tr02", "tr03"] + names("mm13", 0, 3)
+        + names("tr1", 0, 3)
     )
     vector = (
-        ["wr00", "wq00", "wr01", "xq00", "xq01", "vv", "wq01"] + names("xq0", 2, 6)
-        + ["wr10", "xc07", "xq07", "su00", "wr11", "su01", "xc10", "su02", "xc11", "su10", "su11", "xc13"]
-        + ["xq10", "xq11", "xq13", "rd0", "rd1", "rm", "xq12", "wq10", "wq11", "xq14", "mk"]
-        + ["ct00", "ct01", "ct02", "ct10", "mn00", "mn01", "ct03", "xq15", "xq17", "ct11", "xq16", "mn02", "mn03"]
-        + ["ct12", "ct13"] + names("mn1", 0, 3) + ["oc12"]
+        ["wr00", "wq00", "wr01", "wq01", "xq00", "vv", "xq01", "xq02", "am00", "xq03", "am01", "am02", "am03"]
+        + ["wr10", "wq10", "wr11", "wq11", "rs0", "xq10", "rs1", "vm", "xq11", "gm", "mk"]
+        + names("ct0", 0, 3) + ["mn00", "mn01", "xq12", "mn02", "mn03", "xq13"] + names("ct1", 0, 3) + names("mn1", 0, 3)
     )
     scalar = (
-        names("xc0", 0, 6) + ["ab00", "ab01", "ab02", "am00", "am01", "am02", "ab03", "am03"] + names("ab1", 0, 3)
-        + ["am13", "xc12", "xc14", "am10", "am11", "am12", "xc15", "xc16", "xc17"] + names("oc0", 0, 3)
-        + ["oc10", "oc11", "oc13"]
+        names("xc0", 0, 7) + names("ab0", 0, 3) + names("ab1", 0, 3)
+        + ["xc10", "xc11", "am10", "am11", "xc12", "xc13", "am12", "am13"] + names("xc1", 4, 7)
+        + names("oc0", 0, 3) + names("oc1", 0, 3)
     )
     sync = names("st0", 0, 3) + names("st1", 0, 3)
     return tensor, vector, scalar, sync
@@ -59,7 +57,6 @@ def tile_splitnn_pa_kernel(tc, x1, x2, W1, b1, W2, b2, noise_std, rr_uniform, ou
         const = ctx.enter_context(tc.tile_pool(name="const", bufs=1))
         group_pool = ctx.enter_context(tc.tile_pool(name="group_pool", bufs=6))
         abs_pool = ctx.enter_context(tc.tile_pool(name="abs_pool", bufs=8))
-        sum_pool = ctx.enter_context(tc.tile_pool(name="sum_pool", bufs=4))
         min_pool = ctx.enter_context(tc.tile_pool(name="min_pool", bufs=8))
         psum = ctx.enter_context(tc.psum_pool(name="psum", bufs=8))
 
@@ -69,21 +66,13 @@ def tile_splitnn_pa_kernel(tc, x1, x2, W1, b1, W2, b2, noise_std, rr_uniform, ou
         make_identity(nc, ident_bf16[:])
         vector_rows = const.tile([P, P], BF16)
         nc.vector.memset(vector_rows[:], 0.0)
-        plus_minus = const.tile([P, P], F32)
-        nc.vector.memset(plus_minus[:, 0:64], 1.0)
-        nc.vector.memset(plus_minus[:, 64:128], -1.0)
-        pick = const.tile([P, P], F32)
-        nc.vector.memset(pick[:], 0.0)
-        nc.vector.memset(pick[0:1, :], 1.0)
-        nc.vector.memset(pick[64:65, :], 1.0)
+        neg_ident_f32 = const.tile([P, P], F32)
+        nc.vector.tensor_single_scalar(out=neg_ident_f32[:], in_=ident_f32[:], scalar=-1.0, op=ALU.mult)
         zero_column = const.tile([P, 1], F32)
         nc.vector.memset(zero_column[:], 0.0)
         early_abs = const.tile([P, 1], F32)
         nc.scalar.activation(out=early_abs[:], in_=zero_column[:], func=ACT.Abs)
 
-        nc.sync.dma_start(out=vector_rows[0:4, :], in_=b1.rearrange("(r v) -> r v", v=P))
-        nc.sync.dma_start(out=vector_rows[4:8, :], in_=b2.rearrange("(r v) -> r v", v=P))
-        nc.sync.dma_start(out=vector_rows[8:12, :], in_=rr_uniform.rearrange("(r v) -> r v", v=P))
 
         w_raw = [const.tile([P, PASSES, 4, H], BF16, name="w_raw%d" % c) for c in range(2)]
         x_raw = [const.tile([P, BATCH_TILES * F], BF16, name="x_raw%d" % c) for c in range(2)]
@@ -101,6 +90,9 @@ def tile_splitnn_pa_kernel(tc, x1, x2, W1, b1, W2, b2, noise_std, rr_uniform, ou
 
         load_w(0, W1, 0)
         load_x(0, x1, 0)
+        nc.sync.dma_start(out=vector_rows[0:4, :], in_=b1.rearrange("(r v) -> r v", v=P))
+        nc.sync.dma_start(out=vector_rows[4:8, :], in_=b2.rearrange("(r v) -> r v", v=P))
+        nc.sync.dma_start(out=vector_rows[8:12, :], in_=rr_uniform.rearrange("(r v) -> r v", v=P))
         load_w(0, W1, 1)
         for pair in range(1, 4):
             load_x(0, x1, pair)
@@ -113,16 +105,18 @@ def tile_splitnn_pa_kernel(tc, x1, x2, W1, b1, W2, b2, noise_std, rr_uniform, ou
         w_grouped = [const.tile([P, PASSES, H, 4], BF16, name="w_grouped%d" % c, align_bytes=64) for c in range(2)]
         w_words = [const.tile([P, PASSES, H], U32, name="w_words%d" % c, align_bytes=64) for c in range(2)]
         w_scales = [const.tile([P, PASSES, H], U8, name="w_scales%d" % c, align_bytes=64) for c in range(2)]
-        x_words = [const.tile([P, 2, PASSES, HALF], U32, name="x_words%d" % c, align_bytes=64) for c in range(2)]
-        x_scales = [const.tile([P, 2, PASSES, HALF], U8, name="x_scales%d" % c, align_bytes=64) for c in range(2)]
+        x_words = [const.tile([P, 4, PASSES * 2 * P], U32, name="x_words%d" % c, align_bytes=64) for c in range(2)]
+        x_scales = [const.tile([P, 4, PASSES * 2 * P], U8, name="x_scales%d" % c, align_bytes=64) for c in range(2)]
         vectors = const.tile([P, 3 * FEATURE_TILES], F32)
         keep = const.tile([P, FEATURE_TILES], F32)
         b1_kept = const.tile([P, FEATURE_TILES], F32)
         keep_over_eps = const.tile([P, FEATURE_TILES], F32)
         noise_scale = const.tile([P, FEATURE_TILES], F32)
         c_t = const.tile([P, FEATURE_TILES, B], F32)
-        half_max = const.tile([P, 2], F32)
-        both_max = const.tile([P, 2], F32)
+        n_rows = const.tile([P, BATCH_TILES], F32)
+        extremes = const.tile([P, 2], F32)
+        spread = const.tile([P, 2], F32)
+        sens = const.tile([P, 1], F32)
         out_rows = const.tile([P, BATCH_TILES, H], F32)
         out_view = out.rearrange("(p t) j -> p t j", t=BATCH_TILES)
         live = {}
@@ -164,74 +158,80 @@ def tile_splitnn_pa_kernel(tc, x1, x2, W1, b1, W2, b2, noise_std, rr_uniform, ou
 
         def xc(c, i):
             step_name = "xc%d%d" % (c, i)
-            grouped = group_pool.tile([P, 4 * 2 * P], BF16, tag="grouped", align_bytes=64)
-            live[step_name] = grouped
+            pair, g = i // 2, i % 2
+            if "xg%d%d" % (c, pair) not in live:
+                live["xg%d%d" % (c, pair)] = group_pool.tile([P, PASSES * 4 * 2 * P], BF16, tag="grouped", align_bytes=64,
+                                                             name="grouped")
+            grouped = live["xg%d%d" % (c, pair)]
             copy_on_its_engine(step_name)(
-                out=grouped[:].bitcast(F32).rearrange("q (s r u) -> q s r u", s=2, u=2),
+                out=grouped[:, 1024 * g:1024 * (g + 1)].bitcast(F32).rearrange("q (s r u) -> q s r u", s=2, u=2),
                 in_=live["xt%d%d" % (c, i)][:].rearrange("q s u r -> q s r u"),
             )
 
-        def xq(c, i):
-            pair, g = i // 2, i % 2
-            span = slice(2 * P * (pair % 2), 2 * P * (pair % 2 + 1))
+        def xq(c, pair):
             nc.vector.quantize_mx(
-                out=x_words[c][:, pair // 2, g, span].bitcast(FP8X4), scales=x_scales[c][:, pair // 2, g, span],
-                in_=live["xc%d%d" % (c, i)][:],
+                out=x_words[c][:, pair, :].bitcast(FP8X4), scales=x_scales[c][:, pair, :],
+                in_=live["xg%d%d" % (c, pair)][:],
             )
 
-        def mm(c, f, h):
-            acc = psum.tile([P, HALF], F32, tag="bank", name="acc")
-            live["mm%d%d%d" % (c, f, h)] = acc
+        def mm(c, pair, h):
+            f = pair // 2
+            if pair % 2 == 0:
+                live["acc%d%d%d" % (c, f, h)] = psum.tile([P, HALF], F32, tag="bank", name="acc")
+            acc = live["acc%d%d%d" % (c, f, h)]
             features = slice(P * h, P * (h + 1))
             for g in range(PASSES):
+                rows = slice(2 * P * g, 2 * P * (g + 1))
                 nc.tensor.matmul_mx(
-                    out=acc[:],
+                    out=acc[:, 2 * P * (pair % 2):2 * P * (pair % 2 + 1)],
                     lhsT=w_words[c][:, g, features].bitcast(FP8X4), lhsT_scale=w_scales[c][:, g, features],
-                    rhs=x_words[c][:, f, g, :].bitcast(FP8X4), rhs_scale=x_scales[c][:, f, g, :],
+                    rhs=x_words[c][:, pair, rows].bitcast(FP8X4), rhs_scale=x_scales[c][:, pair, rows],
                     start=(g == 0), stop=(g == PASSES - 1),
                 )
 
         def ab(f, h):
             abs_a = abs_pool.tile([P, HALF], F32, tag="abs_a")
             live["ab%d%d" % (f, h)] = abs_a
-            nc.scalar.activation(out=abs_a[:], in_=live["mm0%d%d" % (f, h)][:], func=ACT.Abs,
+            nc.scalar.activation(out=abs_a[:], in_=live["acc0%d%d" % (f, h)][:], func=ACT.Abs,
                                  bias=vectors[:, h:h + 1], scale=1.0)
 
         def am(f, h):
-            nc.scalar.activation(out=c_t[:, h, HALF * f:HALF * (f + 1)], in_=live["mm0%d%d" % (f, h)][:],
-                                 func=ACT.Identity, bias=b1_kept[:, h:h + 1], scale=keep[:, h:h + 1])
+            if "am%d%d" % (f, h) in vector_queue:
+                nc.vector.tensor_scalar(out=c_t[:, h, HALF * f:HALF * (f + 1)], in0=live["acc0%d%d" % (f, h)][:],
+                                        scalar1=keep[:, h:h + 1], scalar2=b1_kept[:, h:h + 1], op0=ALU.mult, op1=ALU.add)
+            else:
+                nc.scalar.activation(out=c_t[:, h, HALF * f:HALF * (f + 1)], in_=live["acc0%d%d" % (f, h)][:],
+                                     func=ACT.Identity, bias=b1_kept[:, h:h + 1], scale=keep[:, h:h + 1])
 
-        sum_inputs = {"su00": ("ab00", "ab01"), "su01": ("su00", "ab02"), "su02": ("su01", "ab03"),
-                      "su10": ("ab10", "ab11"), "su11": ("ab12", "ab13")}
-        n_inputs = {"ns00": ("su02", True, True), "ns10": ("su10", True, False), "ns11": ("su11", False, True)}
+        def ta(f, h):
+            if h == 0:
+                live["ta%d" % f] = psum.tile([P, 4, P], F32, tag="bank", name="abs_rows")
+            for t in range(4):
+                nc.tensor.matmul(out=live["ta%d" % f][:, t, :], lhsT=live["ab%d%d" % (f, h)][:, P * t:P * (t + 1)],
+                                 rhs=ident_f32[:], is_transpose=True,
+                                 start=(h == 0 and t == 0), stop=(h == FEATURE_TILES - 1 and t == 3))
 
-        def su(f, n):
-            step_name = "su%d%d" % (f, n)
-            partial = sum_pool.tile([P, HALF], F32, tag="partial")
-            live[step_name] = partial
-            nc.vector.tensor_tensor(out=partial[:], in0=live[sum_inputs[step_name][0]][:],
-                                    in1=live[sum_inputs[step_name][1]][:], op=ALU.add)
+        def rs(f):
+            nc.vector.tensor_reduce(out=n_rows[:, 4 * f:4 * f + 4], in_=live["ta%d" % f][:], axis=AX.X, op=ALU.add)
 
-        def ns(f, n):
-            source, start, stop = n_inputs["ns%d%d" % (f, n)]
-            if start:
-                live["ns%d" % f] = psum.tile([P, HALF], F32, tag="bank", name="n_signed")
-            nc.tensor.matmul(out=live["ns%d" % f][:], lhsT=plus_minus[:], rhs=live[source][:], start=start, stop=stop)
+        def vm():
+            nc.vector.tensor_reduce(out=extremes[:, 0:1], in_=n_rows[:], axis=AX.X, op=ALU.max)
+            nc.vector.tensor_reduce(out=extremes[:, 1:2], in_=n_rows[:], axis=AX.X, op=ALU.min)
 
-        def rd(f):
-            nc.vector.tensor_reduce(out=half_max[:, f:f + 1], in_=live["ns%d" % f][:], axis=AX.X, op=ALU.max)
+        def bc():
+            live["bc"] = psum.tile([P, 2, P], F32, tag="bank", name="extremes_everywhere")
+            nc.tensor.matmul(out=live["bc"][:, 0, :], lhsT=extremes[:, 0:1].to_broadcast([P, P]), rhs=ident_f32[:],
+                             start=True, stop=True)
+            nc.tensor.matmul(out=live["bc"][:, 1, :], lhsT=extremes[:, 1:2].to_broadcast([P, P]), rhs=neg_ident_f32[:],
+                             start=True, stop=True)
 
-        def rm():
-            nc.vector.tensor_tensor(out=both_max[:], in0=half_max[:, 0:1].to_broadcast([P, 2]),
-                                    in1=half_max[:, 1:2].to_broadcast([P, 2]), op=ALU.max)
-
-        def se():
-            live["se"] = psum.tile([P, 2], F32, tag="bank", name="sens")
-            nc.tensor.matmul(out=live["se"][:], lhsT=pick[:], rhs=both_max[:], start=True, stop=True)
+        def gm():
+            nc.vector.tensor_reduce(out=spread[:], in_=live["bc"][:], axis=AX.X, op=ALU.max)
 
         def mk():
-            nc.vector.tensor_tensor(out=noise_scale[:], in0=live["se"][:, 0:1].to_broadcast([P, FEATURE_TILES]),
-                                    in1=keep_over_eps[:], op=ALU.mult)
+            nc.vector.tensor_tensor(out=sens[:], in0=spread[:, 0:1], in1=spread[:, 1:2], op=ALU.add)
+            nc.vector.tensor_scalar(out=noise_scale[:], in0=keep_over_eps[:], scalar1=sens[:, 0:1], scalar2=None,
+                                    op0=ALU.mult)
 
         def nt(f, p):
             bank = psum.tile([P, 2, HALF], BF16, tag="bank", name="noise_t")
@@ -250,7 +250,7 @@ def tile_splitnn_pa_kernel(tc, x1, x2, W1, b1, W2, b2, noise_std, rr_uniform, ou
         def mn(f, h):
             smaller = min_pool.tile([P, HALF], F32, tag="smaller")
             live["mn%d%d" % (f, h)] = smaller
-            nc.vector.scalar_tensor_tensor(out=smaller[:], in0=live["mm1%d%d" % (f, h)][:],
+            nc.vector.scalar_tensor_tensor(out=smaller[:], in0=live["acc1%d%d" % (f, h)][:],
                                            scalar=vectors[:, 4 + h:5 + h],
                                            in1=c_t[:, h, HALF * f:HALF * (f + 1)], op0=ALU.add, op1=ALU.min)
 
@@ -269,8 +269,8 @@ def tile_splitnn_pa_kernel(tc, x1, x2, W1, b1, W2, b2, noise_std, rr_uniform, ou
             nc.sync.dma_start(out=out_view[:, 4 * f:4 * f + 4, P * h:P * (h + 1)],
                               in_=out_rows[:, 4 * f:4 * f + 4, P * h:P * (h + 1)])
 
-        steps = {"vt": (vt, (), []), "vv": (vv, (), ["vt"]), "rm": (rm, (), ["rd0", "rd1"]), "se": (se, (), ["rm"]),
-                 "mk": (mk, (), ["se", "vv"]), "rd0": (rd, (0,), ["ns00"]), "rd1": (rd, (1,), ["ns11"])}
+        steps = {"vt": (vt, (), []), "vv": (vv, (), ["vt"]), "vm": (vm, (), ["rs0", "rs1"]), "bc": (bc, (), ["vm"]),
+                 "gm": (gm, (), ["bc"]), "mk": (mk, (), ["gm", "vv"]), "rs0": (rs, (0,), ["ta03"]), "rs1": (rs, (1,), ["ta13"])}
         for c in range(2):
             for g in range(PASSES):
                 steps["wr%d%d" % (c, g)] = (wr, (c, g), [])
@@ -278,25 +278,21 @@ def tile_splitnn_pa_kernel(tc, x1, x2, W1, b1, W2, b2, noise_std, rr_uniform, ou
             for i in range(8):
                 steps["xt%d%d" % (c, i)] = (xt, (c, i), [])
                 steps["xc%d%d" % (c, i)] = (xc, (c, i), ["xt%d%d" % (c, i)])
-                steps["xq%d%d" % (c, i)] = (xq, (c, i), ["xc%d%d" % (c, i)])
-            for f in range(2):
-                operands = names("wq%d" % c, 0, 1) + names("xq%d" % c, 4 * f, 4 * f + 3)
+            for pair in range(4):
+                steps["xq%d%d" % (c, pair)] = (xq, (c, pair), names("xc%d" % c, 2 * pair, 2 * pair + 1))
                 for h in range(FEATURE_TILES):
-                    steps["mm%d%d%d" % (c, f, h)] = (mm, (c, f, h), operands)
-        for step_name in sum_inputs:
-            steps[step_name] = (su, (int(step_name[2]), int(step_name[3])), list(sum_inputs[step_name]))
-        for step_name in n_inputs:
-            steps[step_name] = (ns, (int(step_name[2]), int(step_name[3])), [n_inputs[step_name][0]])
-        steps["ns11"][2].append("ns10")
+                    earlier = ["mm%d%d%d" % (c, pair - 1, h)] if pair % 2 else []
+                    steps["mm%d%d%d" % (c, pair, h)] = (mm, (c, pair, h), names("wq%d" % c, 0, 1) + ["xq%d%d" % (c, pair)] + earlier)
         for f in range(2):
             for p in range(2):
                 steps["nt%d%d" % (f, p)] = (nt, (f, p), [])
             for h in range(FEATURE_TILES):
                 fh = "%d%d" % (f, h)
-                steps["ab" + fh] = (ab, (f, h), ["mm0" + fh, "vv"])
-                steps["am" + fh] = (am, (f, h), ["mm0" + fh, "vv"])
+                steps["ab" + fh] = (ab, (f, h), ["mm0%d%d" % (2 * f + 1, h), "vv"])
+                steps["ta" + fh] = (ta, (f, h), ["ab" + fh] + (["ta%d%d" % (f, h - 1)] if h else []))
+                steps["am" + fh] = (am, (f, h), ["mm0%d%d" % (2 * f + 1, h), "vv"])
                 steps["ct" + fh] = (ct, (f, h), ["nt%d%d" % (f, h // 2), "mk", "am" + fh])
-                steps["mn" + fh] = (mn, (f, h), ["mm1" + fh, "ct" + fh])
+                steps["mn" + fh] = (mn, (f, h), ["mm1%d%d" % (2 * f + 1, h), "ct" + fh])
                 steps["tr" + fh] = (tr, (f, h), ["mn" + fh])
                 steps["oc" + fh] = (oc, (f, h), ["tr" + fh])
                 steps["st" + fh] = (st, (f, h), ["oc" + fh])

@@ -29,7 +29,8 @@ def names(prefix, first, last):
 
 def engine_queues():
     tensor = (
-        ["xt00", "xt01", "vt"] + names("xt0", 2, 7) + names("mm00", 0, 3) + names("mm01", 0, 3) + names("mm02", 0, 3)
+        names("du", 0, 7) + ["xt00", "xt01", "vt", "du8", "du9", "xt02", "xt03", "du10", "du11", "xt04", "xt05", "du12", "du13", "xt06", "xt07"]
+        + names("mm00", 0, 3) + names("mm01", 0, 3) + names("mm02", 0, 3)
         + ["ta00", "ta01"] + names("mm03", 0, 3) + ["ta02", "ta03", "xt10", "xt11"] + names("ta1", 0, 3)
         + names("xt1", 2, 5) + ["bc", "nt00", "nt01"] + names("mm10", 0, 3) + names("mm11", 0, 3)
         + ["xt16", "xt17", "nt10", "nt11", "tr00", "tr01"] + names("mm12", 0, 3) + ["tr02", "tr03"] + names("mm13", 0, 3)
@@ -123,6 +124,10 @@ def tile_splitnn_pa_kernel(tc, x1, x2, W1, b1, W2, b2, noise_std, rr_uniform, ou
 
         def copy_on_its_engine(step_name):
             return nc.vector.tensor_copy if step_name in vector_queue else nc.scalar.copy
+
+        def du():
+            scratch = psum.tile([P, P], F32, tag="bank", name="scratch")
+            nc.tensor.matmul(out=scratch[:], lhsT=ident_f32[:], rhs=ident_f32[:], start=True, stop=True)
 
         def vt():
             live["vt"] = psum.tile([P, P], BF16, tag="bank", name="vectors_t")
@@ -271,6 +276,8 @@ def tile_splitnn_pa_kernel(tc, x1, x2, W1, b1, W2, b2, noise_std, rr_uniform, ou
 
         steps = {"vt": (vt, (), []), "vv": (vv, (), ["vt"]), "vm": (vm, (), ["rs0", "rs1"]), "bc": (bc, (), ["vm"]),
                  "gm": (gm, (), ["bc"]), "mk": (mk, (), ["gm", "vv"]), "rs0": (rs, (0,), ["ta03"]), "rs1": (rs, (1,), ["ta13"])}
+        for i in range(14):
+            steps["du%d" % i] = (du, (), [])
         for c in range(2):
             for g in range(PASSES):
                 steps["wr%d%d" % (c, g)] = (wr, (c, g), [])

@@ -184,6 +184,9 @@ def tile_splitnn_pa_kernel(tc, x1, x2, W1, b1, W2, b2, noise_std, rr_uniform, ou
             if pair % 2 == 0:
                 live["acc%d%d%d" % (c, f, h)] = psum.tile([P, HALF], F32, tag="bank", name="acc")
             acc = live["acc%d%d%d" % (c, f, h)]
+            if c == 1 and pair % 2 == 0 and h == 0:
+                for i in range(2):
+                    nc.tensor.matmul(out=acc[:, P * i:P * (i + 1)], lhsT=ident_f32[:], rhs=ident_f32[:], start=True, stop=True)
             features = slice(P * h, P * (h + 1))
             for g in range(PASSES):
                 rows = slice(2 * P * g, 2 * P * (g + 1))

from contextlib import ExitStack

import concourse.mybir as mybir
from concourse.masks import make_identity

F32 = mybir.dt.float32
BF16 = mybir.dt.bfloat16
U32 = mybir.dt.uint32
U8 = mybir.dt.uint8
FP8X4 = mybir.dt.float8_e4m3fn_x4
ALU = mybir.AluOpType
ACT = mybir.ActivationFunctionType
AX = mybir.AxisListType

P = 128
B, F, H = 1024, 1024, 512
FLOPS = 2 * 2 * B * F * H
BATCH_TILES = B // P
PASSES = F // (4 * P)
FEATURE_TILES = H // P
HALF = 512
INV_EPS = 7.5
P_KEEP = 0.95


def names(prefix, first, last):
    return [prefix + str(i) for i in range(first, last + 1)]


def engine_queues():
    tensor = (
        names("du", 0, 7) + ["xt00", "xt01", "vt", "du8", "du9", "xt02", "xt03", "du10", "du11", "xt04", "xt05", "du12", "du13", "xt06", "xt07"]
        + names("mm00", 0, 3) + names("mm01", 0, 3) + names("mm02", 0, 3)
        + ["ta00", "ta01"] + names("mm03", 0, 3) + ["ta02", "ta03", "xt10", "xt11"] + names("ta1", 0, 3)
        + names("xt1", 2, 5) + ["bc", "nt00", "nt01"] + names("mm10", 0, 3) + names("mm11", 0, 3)
        + ["xt16", "xt17", "nt10", "nt11", "tr00", "tr01"] + names("mm12", 0, 3) + ["tr02", "tr03"] + names("mm13", 0, 3)
        + names("tr1", 0, 3)
    )
    vector = (
        ["wr00", "wq00", "wr01", "wq01", "xq00", "vv", "xq01", "xq02", "am00", "xq03", "am01", "am02", "am03"]
        + ["wr10", "wq10", "wr11", "wq11", "rs0", "xq10", "rs1", "vm", "xq11", "gm", "mk"]
        + names("ct0", 0, 3) + ["mn00", "mn01", "xq12", "mn02", "mn03", "xq13"] + names("ct1", 0, 3) + names("mn1", 0, 3)
    )
    scalar = (
        names("xc0", 0, 7) + names("ab0", 0, 3) + names("ab1", 0, 3)
        + ["xc10", "xc11", "am10", "am11", "xc12", "xc13", "am12", "am13"] + names("xc1", 4, 7)
        + names("oc0", 0, 3) + names("oc1", 0, 3)
    )
    sync = names("st0", 0, 3) + names("st1", 0, 3)
    return tensor, vector, scalar, sync


def tile_splitnn_pa_kernel(tc, x1, x2, W1, b1, W2, b2, noise_std, rr_uniform, out):
    nc = tc.nc
    tensor_queue, vector_queue, scalar_queue, sync_queue = engine_queues()
    with ExitStack() as ctx:
        ctx.enter_context(tc.manual_schedule())
        const = ctx.enter_context(tc.tile_pool(name="const", bufs=1))
        group_pool = ctx.enter_context(tc.tile_pool(name="group_pool", bufs=6))
        abs_pool = ctx.enter_context(tc.tile_pool(name="abs_pool", bufs=8))
        min_pool = ctx.enter_context(tc.tile_pool(name="min_pool", bufs=8))
        psum = ctx.enter_context(tc.psum_pool(name="psum", bufs=8))

        ident_f32 = const.tile([P, P], F32)
        make_identity(nc, ident_f32[:])
        ident_bf16 = const.tile([P, P], BF16)
        make_identity(nc, ident_bf16[:])
        vector_rows = const.tile([P, P], BF16)
        nc.vector.memset(vector_rows[:], 0.0)
        neg_ident_f32 = const.tile([P, P], F32)
        nc.vector.tensor_single_scalar(out=neg_ident_f32[:], in_=ident_f32[:], scalar=-1.0, op=ALU.mult)
        zero_column = const.tile([P, 1], F32)
        nc.vector.memset(zero_column[:], 0.0)
        early_abs = const.tile([P, 1], F32)
        nc.scalar.activation(out=early_abs[:], in_=zero_column[:], func=ACT.Abs)


        w_raw = [const.tile([P, PASSES, 4, H], BF16, name="w_raw%d" % c) for c in range(2)]
        x_raw = [const.tile([P, BATCH_TILES * F], BF16, name="x_raw%d" % c) for c in range(2)]
        noise = const.tile([P, BATCH_TILES, H], BF16)

        def load_w(c, w, g):
            nc.sync.dma_start(
                out=w_raw[c][:, g].rearrange("q (u e) j -> q u (e j)", u=2),
                in_=w[512 * g:512 * (g + 1), :].rearrange("(u q e) j -> q u (e j)", u=2, e=2),
            )

        def load_x(c, x, pair):
            span = slice(2 * F * pair, 2 * F * (pair + 1))
            nc.sync.dma_start(out=x_raw[c][:, span], in_=x.rearrange("(p t) k -> p (t k)", t=BATCH_TILES)[:, span])

        load_w(0, W1, 0)
        load_x(0, x1, 0)
        nc.sync.dma_start(out=vector_rows[0:4, :], in_=b1.rearrange("(r v) -> r v", v=P))
        nc.sync.dma_start(out=vector_rows[4:8, :], in_=b2.rearrange("(r v) -> r v", v=P))
        nc.sync.dma_start(out=vector_rows[8:12, :], in_=rr_uniform.rearrange("(r v) -> r v", v=P))
        load_w(0, W1, 1)
        for pair in range(1, 4):
            load_x(0, x1, pair)
        load_w(1, W2, 0)
        load_w(1, W2, 1)
        for pair in range(4):
            load_x(1, x2, pair)
        nc.sync.dma_start(out=noise[:], in_=noise_std.rearrange("(p t) j -> p t j", t=BATCH_TILES))

        w_grouped = [const.tile([P, PASSES, H, 4], BF16, name="w_grouped%d" % c, align_bytes=64) for c in range(2)]
        w_words = [const.tile([P, PASSES, H], U32, name="w_words%d" % c, align_bytes=64) for c in range(2)]
        w_scales = [const.tile([P, PASSES, H], U8, name="w_scales%d" % c, align_bytes=64) for c in range(2)]
        x_words = [const.tile([P, 4, PASSES * 2 * P], U32, name="x_words%d" % c, align_bytes=64) for c in range(2)]
        x_scales = [const.tile([P, 4, PASSES * 2 * P], U8, name="x_scales%d" % c, align_bytes=64) for c in range(2)]
        vectors = const.tile([P, 3 * FEATURE_TILES], F32)
        keep = const.tile([P, FEATURE_TILES], F32)
        b1_kept = const.tile([P, FEATURE_TILES], F32)
        keep_over_eps = const.tile([P, FEATURE_TILES], F32)
        noise_scale = const.tile([P, FEATURE_TILES], F32)
        c_t = const.tile([P, FEATURE_TILES, B], F32)
        n_rows = const.tile([P, BATCH_TILES], F32)
        extremes = const.tile([P, 2], F32)
        spread = const.tile([P, 2], F32)
        sens = const.tile([P, 1], F32)
        out_rows = const.tile([P, BATCH_TILES, H], F32)
        out_view = out.rearrange("(p t) j -> p t j", t=BATCH_TILES)
        live = {}

        def copy_on_its_engine(step_name):
            return nc.vector.tensor_copy if step_name in vector_queue else nc.scalar.copy

        def du():
            scratch = psum.tile([P, P], F32, tag="bank", name="scratch")
            nc.tensor.matmul(out=scratch[:], lhsT=ident_f32[:], rhs=ident_f32[:], start=True, stop=True)

        def vt():
            live["vt"] = psum.tile([P, P], BF16, tag="bank", name="vectors_t")
            nc.tensor.transpose(live["vt"][:], vector_rows[:], ident_bf16[:])

        def vv():
            nc.vector.tensor_copy(out=vectors[:], in_=live["vt"][:, 0:3 * FEATURE_TILES])
            nc.vector.tensor_single_scalar(out=keep[:], in_=vectors[:, 8:12], scalar=P_KEEP, op=ALU.is_lt)
            nc.vector.tensor_tensor(out=b1_kept[:], in0=vectors[:, 0:4], in1=keep[:], op=ALU.mult)
            nc.vector.tensor_single_scalar(out=keep_over_eps[:], in_=keep[:], scalar=INV_EPS, op=ALU.mult)

        def wr(c, g):
            nc.vector.tensor_copy(
                out=w_grouped[c][:, g].rearrange("q (n i) v -> q n v i", i=4),
                in_=w_raw[c][:, g].rearrange("q v (n i) -> q n v i", i=4),
            )

        def wq(c, g):
            nc.vector.quantize_mx(
                out=w_words[c][:, g, :].bitcast(FP8X4), scales=w_scales[c][:, g, :],
                in_=w_grouped[c][:, g].rearrange("q j v -> q (j v)"),
            )

        def xt(c, i):
            pair, g = i // 2, i % 2
            words = x_raw[c][:].bitcast(F32)
            bank = psum.tile([P, 2, 2, P], F32, tag="bank", name="x_t")
            live["xt%d%d" % (c, i)] = bank
            for s in range(2):
                for u in range(2):
                    first = (F // 2) * (2 * pair + s) + 256 * g + P * u
                    nc.tensor.transpose(bank[:, s, u, :], words[:, first:first + P], ident_f32[:])

        def xc(c, i):
            step_name = "xc%d%d" % (c, i)
            pair, g = i // 2, i % 2
            if "xg%d%d" % (c, pair) not in live:
                live["xg%d%d" % (c, pair)] = group_pool.tile([P, PASSES * 4 * 2 * P], BF16, tag="grouped", align_bytes=64,
                                                             name="grouped")
            grouped = live["xg%d%d" % (c, pair)]
            copy_on_its_engine(step_name)(
                out=grouped[:, 1024 * g:1024 * (g + 1)].bitcast(F32).rearrange("q (s r u) -> q s r u", s=2, u=2),
                in_=live["xt%d%d" % (c, i)][:].rearrange("q s u r -> q s r u"),
            )

        def xq(c, pair):
            nc.vector.quantize_mx(
                out=x_words[c][:, pair, :].bitcast(FP8X4), scales=x_scales[c][:, pair, :],
                in_=live["xg%d%d" % (c, pair)][:],
            )

        def mm(c, pair, h):
            f = pair // 2
            if pair % 2 == 0:
                live["acc%d%d%d" % (c, f, h)] = psum.tile([P, HALF], F32, tag="bank", name="acc")
            acc = live["acc%d%d%d" % (c, f, h)]
            if c == 1 and pair % 2 == 0 and h == 0:
                for i in range(2):
                    nc.tensor.matmul(out=acc[:, P * i:P * (i + 1)], lhsT=ident_f32[:], rhs=ident_f32[:], start=True, stop=True)
            features = slice(P * h, P * (h + 1))
            for g in range(PASSES):
                rows = slice(2 * P * g, 2 * P * (g + 1))
                nc.tensor.matmul_mx(
                    out=acc[:, 2 * P * (pair % 2):2 * P * (pair % 2 + 1)],
                    lhsT=w_words[c][:, g, features].bitcast(FP8X4), lhsT_scale=w_scales[c][:, g, features],
                    rhs=x_words[c][:, pair, rows].bitcast(FP8X4), rhs_scale=x_scales[c][:, pair, rows],
                    start=(g == 0), stop=(g == PASSES - 1),
                )

        def ab(f, h):
            abs_a = abs_pool.tile([P, HALF], F32, tag="abs_a")
            live["ab%d%d" % (f, h)] = abs_a
            nc.scalar.activation(out=abs_a[:], in_=live["acc0%d%d" % (f, h)][:], func=ACT.Abs,
                                 bias=vectors[:, h:h + 1], scale=1.0)

        def am(f, h):
            if "am%d%d" % (f, h) in vector_queue:
                nc.vector.tensor_scalar(out=c_t[:, h, HALF * f:HALF * (f + 1)], in0=live["acc0%d%d" % (f, h)][:],
                                        scalar1=keep[:, h:h + 1], scalar2=b1_kept[:, h:h + 1], op0=ALU.mult, op1=ALU.add)
            else:
                nc.scalar.activation(out=c_t[:, h, HALF * f:HALF * (f + 1)], in_=live["acc0%d%d" % (f, h)][:],
                                     func=ACT.Identity, bias=b1_kept[:, h:h + 1], scale=keep[:, h:h + 1])

        def ta(f, h):
            if h == 0:
                live["ta%d" % f] = psum.tile([P, 4, P], F32, tag="bank", name="abs_rows")
            for t in range(4):
                nc.tensor.matmul(out=live["ta%d" % f][:, t, :], lhsT=live["ab%d%d" % (f, h)][:, P * t:P * (t + 1)],
                                 rhs=ident_f32[:], is_transpose=True,
                                 start=(h == 0 and t == 0), stop=(h == FEATURE_TILES - 1 and t == 3))

        def rs(f):
            nc.vector.tensor_reduce(out=n_rows[:, 4 * f:4 * f + 4], in_=live["ta%d" % f][:], axis=AX.X, op=ALU.add)

        def vm():
            nc.vector.tensor_reduce(out=extremes[:, 0:1], in_=n_rows[:], axis=AX.X, op=ALU.max)
            nc.vector.tensor_reduce(out=extremes[:, 1:2], in_=n_rows[:], axis=AX.X, op=ALU.min)

        def bc():
            live["bc"] = psum.tile([P, 2, P], F32, tag="bank", name="extremes_everywhere")
            nc.tensor.matmul(out=live["bc"][:, 0, :], lhsT=extremes[:, 0:1].to_broadcast([P, P]), rhs=ident_f32[:],
                             start=True, stop=True)
            nc.tensor.matmul(out=live["bc"][:, 1, :], lhsT=extremes[:, 1:2].to_broadcast([P, P]), rhs=neg_ident_f32[:],
                             start=True, stop=True)

        def gm():
            nc.vector.tensor_reduce(out=spread[:], in_=live["bc"][:], axis=AX.X, op=ALU.max)

        def mk():
            nc.vector.tensor_tensor(out=sens[:], in0=spread[:, 0:1], in1=spread[:, 1:2], op=ALU.add)
            nc.vector.tensor_scalar(out=noise_scale[:], in0=keep_over_eps[:], scalar1=sens[:, 0:1], scalar2=None,
                                    op0=ALU.mult)

        def nt(f, p):
            bank = psum.tile([P, 2, HALF], BF16, tag="bank", name="noise_t")
            live["nt%d%d" % (f, p)] = bank
            for s in range(2):
                h = 2 * p + s
                for t in range(4):
                    nc.tensor.transpose(bank[:, s, P * t:P * (t + 1)],
                                        noise[:, 4 * f + t, P * h:P * (h + 1)], ident_bf16[:])

        def ct(f, h):
            part = c_t[:, h, HALF * f:HALF * (f + 1)]
            nc.vector.scalar_tensor_tensor(out=part, in0=live["nt%d%d" % (f, h // 2)][:, h % 2, :],
                                           scalar=noise_scale[:, h:h + 1], in1=part, op0=ALU.mult, op1=ALU.add)

        def mn(f, h):
            smaller = min_pool.tile([P, HALF], F32, tag="smaller")
            live["mn%d%d" % (f, h)] = smaller
            nc.vector.scalar_tensor_tensor(out=smaller[:], in0=live["acc1%d%d" % (f, h)][:],
                                           scalar=vectors[:, 4 + h:5 + h],
                                           in1=c_t[:, h, HALF * f:HALF * (f + 1)], op0=ALU.add, op1=ALU.min)

        def tr(f, h):
            bank = psum.tile([P, 4, P], F32, tag="bank", name="out_t")
            live["tr%d%d" % (f, h)] = bank
            for t in range(4):
                nc.tensor.transpose(bank[:, t, :], live["mn%d%d" % (f, h)][:, P * t:P * (t + 1)], ident_f32[:])

        def oc(f, h):
            copy_on_its_engine("oc%d%d" % (f, h))(
                out=out_rows[:, 4 * f:4 * f + 4, P * h:P * (h + 1)], in_=live["tr%d%d" % (f, h)][:]
            )

        def st(f, h):
            nc.sync.dma_start(out=out_view[:, 4 * f:4 * f + 4, P * h:P * (h + 1)],
                              in_=out_rows[:, 4 * f:4 * f + 4, P * h:P * (h + 1)])

        steps = {"vt": (vt, (), []), "vv": (vv, (), ["vt"]), "vm": (vm, (), ["rs0", "rs1"]), "bc": (bc, (), ["vm"]),
                 "gm": (gm, (), ["bc"]), "mk": (mk, (), ["gm", "vv"]), "rs0": (rs, (0,), ["ta03"]), "rs1": (rs, (1,), ["ta13"])}
        for i in range(14):
            steps["du%d" % i] = (du, (), [])
        for c in range(2):
            for g in range(PASSES):
                steps["wr%d%d" % (c, g)] = (wr, (c, g), [])
                steps["wq%d%d" % (c, g)] = (wq, (c, g), ["wr%d%d" % (c, g)])
            for i in range(8):
                steps["xt%d%d" % (c, i)] = (xt, (c, i), [])
                steps["xc%d%d" % (c, i)] = (xc, (c, i), ["xt%d%d" % (c, i)])
            for pair in range(4):
                steps["xq%d%d" % (c, pair)] = (xq, (c, pair), names("xc%d" % c, 2 * pair, 2 * pair + 1))
                for h in range(FEATURE_TILES):
                    earlier = ["mm%d%d%d" % (c, pair - 1, h)] if pair % 2 else []
                    steps["mm%d%d%d" % (c, pair, h)] = (mm, (c, pair, h), names("wq%d" % c, 0, 1) + ["xq%d%d" % (c, pair)] + earlier)
        for f in range(2):
            for p in range(2):
                steps["nt%d%d" % (f, p)] = (nt, (f, p), [])
            for h in range(FEATURE_TILES):
                fh = "%d%d" % (f, h)
                steps["ab" + fh] = (ab, (f, h), ["mm0%d%d" % (2 * f + 1, h), "vv"])
                steps["ta" + fh] = (ta, (f, h), ["ab" + fh] + (["ta%d%d" % (f, h - 1)] if h else []))
                steps["am" + fh] = (am, (f, h), ["mm0%d%d" % (2 * f + 1, h), "vv"])
                steps["ct" + fh] = (ct, (f, h), ["nt%d%d" % (f, h // 2), "mk", "am" + fh])
                steps["mn" + fh] = (mn, (f, h), ["mm1%d%d" % (2 * f + 1, h), "ct" + fh])
                steps["tr" + fh] = (tr, (f, h), ["mn" + fh])
                steps["oc" + fh] = (oc, (f, h), ["tr" + fh])
                steps["st" + fh] = (st, (f, h), ["oc" + fh])

        queues = [tensor_queue, vector_queue, scalar_queue, sync_queue]
        assert sorted(tensor_queue + vector_queue + scalar_queue + sync_queue) == sorted(steps)
        heads = [0, 0, 0, 0]
        written = set()
        while len(written) < len(steps):
            before = len(written)
            for turn in range(4):
                queue = queues[turn]
                while heads[turn] < len(queue) and all(need in written for need in steps[queue[heads[turn]]][2]):
                    function, arguments, needs = steps[queue[heads[turn]]]
                    function(*arguments)
                    written.add(queue[heads[turn]])
                    heads[turn] += 1
            assert len(written) > before, "the queues wait for each other"
